import numpy as np
import ml_dtypes


def mxq(x, axis, fmt="e4m3"):
    dtype, down = {"e4m3": (ml_dtypes.float8_e4m3fn, 7), "e5m2": (ml_dtypes.float8_e5m2, 14)}[fmt]
    v = np.moveaxis(np.asarray(x, np.float32).astype(ml_dtypes.bfloat16).astype(np.float64), axis, -1)
    blocks = v.reshape(v.shape[:-1] + (-1, 32))
    amax = np.abs(blocks).max(-1, keepdims=True)
    byte = np.maximum(np.where(amax > 0, np.frexp(amax)[1] - 1 + 127, 0) - down, 1)
    scale = np.exp2(byte - 127.0)
    codes = (blocks / scale).astype(np.float32).astype(dtype).astype(np.float64)
    return np.moveaxis((codes * scale).reshape(v.shape), -1, axis)


WIDE = False


def mx_kscale(k):
    if not WIDE:
        return np.ones(k)
    levels = np.array([10, -10, 5, -5, 0])
    a = np.random.permutation(np.resize(levels, k // 512 * 4)).reshape(k // 512, 4)
    idx = np.arange(k)
    return np.exp2(a[idx // 512, idx % 128 // 32])


BF16 = ml_dtypes.bfloat16


def bf(x):
    return np.asarray(x, np.float32).astype(BF16)


def f64(x):
    return np.asarray(x).astype(np.float64)


B, F, DEPTH, T, DO = 8192, 512, 4, 64, 512
L = 2 ** DEPTH


def sigmoid(v):
    return 1.0 / (1.0 + np.exp(-v))


def setup_inputs():
    s = mx_kscale(F)
    return {"x": bf(np.random.standard_normal((B, F)) * s),
            "W": bf(np.random.standard_normal((DEPTH, F, T)) * 1.5 / np.sqrt(F) / s[None, :, None]),
            "b": bf(np.random.standard_normal((DEPTH, T)) * 0.5),
            "leaf_values": bf(np.random.standard_normal((T, L, DO)) * np.sqrt(T))}


def reference(x, W, b, leaf_values):
    z = mxq(f64(x), 1, "e4m3") @ mxq(f64(W), 1, "e4m3")
    split_probs = sigmoid(z.transpose(1, 0, 2) + f64(b))
    leaf_ids = np.arange(L)
    path_probs = np.ones((x.shape[0], T, L))
    for level in range(DEPTH):
        bit = (leaf_ids >> (DEPTH - level - 1)) & 1
        p = split_probs[:, level, :, None]
        path_probs = path_probs * np.where(bit == 0, p, 1.0 - p)
    pq = mxq(path_probs.reshape(-1, T * L), 1, "e4m3")
    lq = mxq(f64(leaf_values).reshape(T * L, DO), 0, "e4m3")
    return (pq @ lq) / T

@@ -1,0 +1,286 @@
+from contextlib import ExitStack
+
+import concourse.mybir as mybir
+from concourse.masks import make_identity
+
+F32 = mybir.dt.float32
+BF16 = mybir.dt.bfloat16
+U32 = mybir.dt.uint32
+I32 = mybir.dt.int32
+U8 = mybir.dt.uint8
+FP8X4 = mybir.dt.float8_e4m3fn_x4
+ACT = mybir.ActivationFunctionType
+ALU = mybir.AluOpType
+
+P = 128
+ROWS = 8192
+FEAT = 512
+DEPTH = 4
+TREES = 64
+LEAVES = 16
+DOUT = 512
+HALF = ROWS // 2
+NB = 256
+R = NB // P
+NBLK = HALF // NB
+PIN = False
+LEAF_AT = 2
+
+FLOPS = 2 * ROWS * FEAT * DEPTH * TREES + 2 * ROWS * TREES * LEAVES * DOUT
+
+
+def tile_neuralobliviousdecisiontree_t_kernel(tc, x, W, b, leaf_values, out):
+    nc = tc.nc
+    with ExitStack() as ctx:
+        if PIN:
+            ctx.enter_context(tc.manual_schedule())
+        const = ctx.enter_context(tc.tile_pool(name="const", bufs=1))
+        xr_pool = ctx.enter_context(tc.tile_pool(name="xr", bufs=4))
+        gx_pool = ctx.enter_context(tc.tile_pool(name="gx", bufs=2))
+        cx_pool = ctx.enter_context(tc.tile_pool(name="cx", bufs=2))
+        q_pool = ctx.enter_context(tc.tile_pool(name="q", bufs=2))
+        ab_pool = ctx.enter_context(tc.tile_pool(name="ab", bufs=2))
+        pa_pool = ctx.enter_context(tc.tile_pool(name="pa", bufs=2))
+        pc_pool = ctx.enter_context(tc.tile_pool(name="pc", bufs=4))
+        o_pool = ctx.enter_context(tc.tile_pool(name="o", bufs=4))
+        ps_x = ctx.enter_context(tc.psum_pool(name="psx", bufs=2))
+        ps_z = ctx.enter_context(tc.psum_pool(name="psz", bufs=4))
+        ps_o = ctx.enter_context(tc.psum_pool(name="pso", bufs=2))
+
+        x_blk = x.rearrange("(h k p r) f -> k p h (r f)", h=2, k=NBLK, p=P, r=R)
+
+        xr_t = {}
+        gx_t = {}
+        cx_t = {}
+        q_t = {}
+        ab_t = {}
+        pc_t = {}
+        o_t = {}
+
+        def load_x(k):
+            xr = xr_pool.tile([P, 2, R * FEAT], BF16, name="xr")
+            nc.sync.dma_start(out=xr[:], in_=x_blk[k])
+            xr_t[k] = xr
+
+        lr = const.tile([P, LEAVES, DOUT], BF16, name="lr")
+        nc.scalar.dma_start(out=lr[0:TREES], in_=leaf_values)
+        nc.scalar.dma_start(out=lr[TREES : 2 * TREES], in_=leaf_values)
+        ident = const.tile([P, P], F32, name="ident")
+        make_identity(nc, ident[:])
+
+        wr = const.tile([P, DEPTH, 4, TREES], BF16, name="wr")
+        nc.sync.dma_start(
+            out=wr[:].rearrange("q j (u e) t -> q (j u) (e t)", u=2, e=2),
+            in_=W.rearrange("j (u q e) t -> q (j u) (e t)", u=2, q=P, e=2),
+        )
+        bt = const.tile([P, P], BF16, name="bt")
+        nc.vector.memset(bt[:], 0.0)
+        nc.sync.dma_start(out=bt[0:DEPTH, 0:TREES], in_=b)
+        nc.sync.dma_start(out=bt[0:DEPTH, TREES : 2 * TREES], in_=b)
+        load_x(0)
+        load_x(1)
+        load_x(2)
+
+        wg = const.tile([P, 2, DEPTH, P, 4], BF16, name="wg", align_bytes=64)
+        nc.vector.memset(wg[:].rearrange("q v j m c -> q (v j m c)").bitcast(I32), 0)
+        lc = const.tile([P, 2, 4, DOUT], U32, name="lc", align_bytes=64)
+        ls = const.tile([P, 4, DOUT], U8, name="ls", align_bytes=64)
+        nc.vector.memset(lc[0:TREES, 1].bitcast(I32), 0)
+
+        for v in range(2):
+            nc.vector.tensor_copy(
+                out=wg[:, v, :, v * TREES : (v + 1) * TREES, :],
+                in_=wr[:].rearrange("q j c t -> q j t c"),
+            )
+        wc = const.tile([P, 2 * DEPTH * P], U32, name="wc", align_bytes=64)
+        ws = const.tile([P, 2 * DEPTH * P], U8, name="ws", align_bytes=64)
+        nc.vector.quantize_mx(
+            out=wc[:].bitcast(FP8X4),
+            scales=ws[:],
+            in_=wg[:].rearrange("q v j m c -> q (v j m c)"),
+        )
+
+        btf = const.tile([P, P], F32, name="btf")
+        nc.vector.tensor_copy(out=btf[:], in_=bt[:])
+        pb = ps_x.tile([P, P], F32, name="pb", tag="xt")
+        nc.tensor.transpose(pb[:], btf[:], ident[:])
+        bpos = const.tile([P, DEPTH], F32, name="bpos")
+        bneg = const.tile([P, DEPTH], F32, name="bneg")
+        nc.vector.tensor_copy(out=bpos[:], in_=pb[:, 0:DEPTH])
+        nc.vector.tensor_scalar(
+            out=bneg[:], in0=pb[:, 0:DEPTH], scalar1=-1.0, scalar2=None, op0=ALU.mult
+        )
+
+        lg = const.tile([P, 4, DOUT, 4], BF16, name="lg", align_bytes=64)
+
+        def leaf_regroup(a):
+            nc.scalar.copy(
+                out=lg[:, a].rearrange("p (c i) t -> p c t i", i=4),
+                in_=lr[:, 4 * a : 4 * a + 4, :].rearrange("p t (c i) -> p c t i", i=4),
+            )
+
+        def leaf_quant():
+            for g in range(2):
+                nc.vector.quantize_mx(
+                    out=lc[:, 0, 2 * g : 2 * g + 2, :].rearrange("p a d -> p (a d)").bitcast(FP8X4),
+                    scales=ls[:, 2 * g : 2 * g + 2, :].rearrange("p a d -> p (a d)"),
+                    in_=lg[:, 2 * g : 2 * g + 2].rearrange("p a d i -> p (a d i)"),
+                )
+            nc.vector.tensor_copy(
+                out=lc[TREES : 2 * TREES, 1].bitcast(I32),
+                in_=lc[TREES : 2 * TREES, 0].bitcast(I32),
+            )
+            nc.vector.memset(lc[TREES : 2 * TREES, 0].bitcast(I32), 0)
+
+        def transpose_x(k):
+            xr = xr_t[k]
+            gx = gx_pool.tile([P, 2, NB, 4], BF16, name="gx", align_bytes=64)
+            for h in range(2):
+                xt = ps_x.tile([P, R, 2, P], F32, name="xt", tag="xt")
+                xw = xr[:, h, :].bitcast(F32)
+                for r in range(R):
+                    for u in range(2):
+                        c0 = r * (FEAT // 2) + u * P
+                        nc.tensor.transpose(xt[:, r, u, :], xw[:, c0 : c0 + P], ident[:])
+                nc.scalar.copy(
+                    out=gx[:, h].bitcast(F32).rearrange("q (r p) u -> q r p u", r=R),
+                    in_=xt[:].rearrange("q r u p -> q r p u"),
+                )
+            gx_t[k] = gx
+
+        def quant_x(k):
+            gx = gx_t[k]
+            cx = cx_pool.tile([P, 2, NB], U32, name="cx", align_bytes=64)
+            sx = cx_pool.tile([P, 2, NB], U8, name="sx", align_bytes=64)
+            nc.vector.quantize_mx(
+                out=cx[:].rearrange("q h n -> q (h n)").bitcast(FP8X4),
+                scales=sx[:].rearrange("q h n -> q (h n)"),
+                in_=gx[:].rearrange("q h n c -> q (h n c)"),
+            )
+            cx_t[k] = (cx, sx)
+
+        def stage1(k):
+            cx, sx = cx_t[k]
+            q = q_pool.tile([P, DEPTH, 2, NB], F32, name="q")
+            for jp in range(DEPTH // 2):
+                z = ps_z.tile([P, 2, NB], F32, name="z")
+                for jj in range(2):
+                    j = 2 * jp + jj
+                    for v in range(2):
+                        w0 = (v * DEPTH + j) * P
+                        nc.tensor.matmul_mx(
+                            out=z[:, jj, :],
+                            lhsT=wc[:, w0 : w0 + P].bitcast(FP8X4),
+                            lhsT_scale=ws[:, w0 : w0 + P],
+                            rhs=cx[:, v, :].bitcast(FP8X4),
+                            rhs_scale=sx[:, v, :],
+                            start=(v == 0),
+                            stop=(v == 1),
+                        )
+                for jj in range(2):
+                    j = 2 * jp + jj
+                    nc.scalar.activation(
+                        out=q[:, j, 0, :], in_=z[:, jj, :], func=ACT.Sigmoid,
+                        bias=bpos[:, j : j + 1], scale=1.0,
+                    )
+                    nc.scalar.activation(
+                        out=q[:, j, 1, :], in_=z[:, jj, :], func=ACT.Sigmoid,
+                        bias=bneg[:, j : j + 1], scale=-1.0,
+                    )
+            q_t[k] = q
+
+        def products(k):
+            q = q_t[k]
+            at = ab_pool.tile([P, 2, 2, NB], F32, name="at")
+            bb = ab_pool.tile([P, NB, 2, 2], F32, name="bb")
+            nc.vector.tensor_tensor(
+                out=at[:],
+                in0=q[:, 0].unsqueeze(2).to_broadcast([P, 2, 2, NB]),
+                in1=q[:, 1].unsqueeze(1).to_broadcast([P, 2, 2, NB]),
+                op=ALU.mult,
+            )
+            nc.vector.tensor_tensor(
+                out=bb[:],
+                in0=q[:, 2].rearrange("p s n -> p n s").unsqueeze(3).to_broadcast([P, NB, 2, 2]),
+                in1=q[:, 3].rearrange("p s n -> p n s").unsqueeze(2).to_broadcast([P, NB, 2, 2]),
+                op=ALU.mult,
+            )
+            pa = pa_pool.tile([P, R, 4, P, 4], BF16, name="pa", align_bytes=64)
+            for r in range(R):
+                cols = slice(r * P, (r + 1) * P)
+                nc.vector.tensor_tensor(
+                    out=pa[:, r],
+                    in0=at[:].rearrange("p s c n -> p (s c) n")[:, :, cols].unsqueeze(3).to_broadcast([P, 4, P, 4]),
+                    in1=bb[:].rearrange("p n s c -> p n (s c)")[:, cols, :].unsqueeze(1).to_broadcast([P, 4, P, 4]),
+                    op=ALU.mult,
+                )
+            pc = pc_pool.tile([P, R, 4, P], U32, name="pc", align_bytes=64)
+            ps = pc_pool.tile([P, R, 4, P], U8, name="ps", align_bytes=64)
+            ab_t[k] = pa
+            pc_t[k] = (pc, ps)
+
+        def quant_path(k, r):
+            pa = ab_t[k]
+            pc, ps = pc_t[k]
+            nc.vector.quantize_mx(
+                out=pc[:, r].rearrange("p a n -> p (a n)").bitcast(FP8X4),
+                scales=ps[:, r].rearrange("p a n -> p (a n)"),
+                in_=pa[:, r].rearrange("p a n i -> p (a n i)"),
+            )
+
+        def stage2(k, r):
+            pc, ps = pc_t[k]
+            if r == 0:
+                o_t[k] = [o_pool.tile([P, R, DOUT], F32, name="o") for h in range(2)]
+            for h in range(2):
+                o = o_t[k][h]
+                acc = ps_o.tile([P, DOUT], F32, name="acc")
+                for a in range(4):
+                    nc.tensor.matmul_mx(
+                        out=acc[:],
+                        lhsT=pc[:, r, a, :].bitcast(FP8X4),
+                        lhsT_scale=ps[:, r, a, :],
+                        rhs=lc[:, h, a, :].bitcast(FP8X4),
+                        rhs_scale=ls[:, a, :],
+                        start=(a == 0),
+                        stop=(a == 3),
+                    )
+                nc.scalar.activation(
+                    out=o[:, r, :], in_=acc[:], func=ACT.Copy, scale=1.0 / TREES
+                )
+                if r == R - 1:
+                    row0 = h * HALF + k * NB
+                    nc.sync.dma_start(
+                        out=out[row0 : row0 + NB, :].rearrange("(p r) d -> p r d", r=R),
+                        in_=o[:],
+                    )
+
+        units = []
+        for k in range(-3, NBLK + 1):
+            if 3 <= k + 6 < NBLK:
+                load_x(k + 6)
+            if 0 <= k + 1 < NBLK:
+                stage1(k + 1)
+            if 0 <= k < 2:
+                leaf_regroup(2 * k)
+                leaf_regroup(2 * k + 1)
+            if 0 <= k < NBLK:
+                products(k)
+                quant_path(k, 0)
+            if 0 <= k + 2 < NBLK:
+                quant_x(k + 2)
+            if 0 <= k < NBLK:
+                quant_path(k, 1)
+            if k == LEAF_AT:
+                leaf_quant()
+            if 0 <= k - 1 < NBLK:
+                units.append((k - 1, 1))
+            if 0 <= k < NBLK:
+                units.append((k, 0))
+            if k >= LEAF_AT:
+                for kk, r in units[:3]:
+                    stage2(kk, r)
+                units = units[3:]
+            if 0 <= k + 3 < NBLK:
+                transpose_x(k + 3)
+        assert len(units) == 0

@@ -23,7 +23,7 @@ HALF = ROWS // 2
 NB = 256
 R = NB // P
 NBLK = HALF // NB
-PIN = False
+PIN = True
 LEAF_AT = 2
 
 FLOPS = 2 * ROWS * FEAT * DEPTH * TREES + 2 * ROWS * TREES * LEAVES * DOUT

@@ -23,8 +23,11 @@ HALF = ROWS // 2
 NB = 256
 R = NB // P
 NBLK = HALF // NB
-PIN = True
+PIN = False
 LEAF_AT = 2
+PSUM_R = (0, 1)
+A_ON_G = True
+B_ON_G = True
 
 FLOPS = 2 * ROWS * FEAT * DEPTH * TREES + 2 * ROWS * TREES * LEAVES * DOUT
 
@@ -39,12 +42,14 @@ def tile_neuralobliviousdecisiontree_t_kernel(tc, x, W, b, leaf_values, out):
         gx_pool = ctx.enter_context(tc.tile_pool(name="gx", bufs=2))
         cx_pool = ctx.enter_context(tc.tile_pool(name="cx", bufs=2))
         q_pool = ctx.enter_context(tc.tile_pool(name="q", bufs=2))
-        ab_pool = ctx.enter_context(tc.tile_pool(name="ab", bufs=2))
+        ab_pool = ctx.enter_context(tc.tile_pool(name="ab", bufs=4))
+        an_pool = ctx.enter_context(tc.tile_pool(name="an", bufs=2))
         pa_pool = ctx.enter_context(tc.tile_pool(name="pa", bufs=2))
         pc_pool = ctx.enter_context(tc.tile_pool(name="pc", bufs=4))
         o_pool = ctx.enter_context(tc.tile_pool(name="o", bufs=4))
         ps_x = ctx.enter_context(tc.psum_pool(name="psx", bufs=2))
-        ps_z = ctx.enter_context(tc.psum_pool(name="psz", bufs=4))
+        ps_z = ctx.enter_context(tc.psum_pool(name="psz", bufs=2))
+        ps_a = ctx.enter_context(tc.psum_pool(name="psa", bufs=2))
         ps_o = ctx.enter_context(tc.psum_pool(name="pso", bufs=2))
 
         x_blk = x.rearrange("(h k p r) f -> k p h (r f)", h=2, k=NBLK, p=P, r=R)
@@ -56,15 +61,15 @@ def tile_neuralobliviousdecisiontree_t_kernel(tc, x, W, b, leaf_values, out):
         ab_t = {}
         pc_t = {}
         o_t = {}
+        f_t = {}
+        an_t = {}
+        a2_t = {}
 
         def load_x(k):
             xr = xr_pool.tile([P, 2, R * FEAT], BF16, name="xr")
             nc.sync.dma_start(out=xr[:], in_=x_blk[k])
             xr_t[k] = xr
 
-        lr = const.tile([P, LEAVES, DOUT], BF16, name="lr")
-        nc.scalar.dma_start(out=lr[0:TREES], in_=leaf_values)
-        nc.scalar.dma_start(out=lr[TREES : 2 * TREES], in_=leaf_values)
         ident = const.tile([P, P], F32, name="ident")
         make_identity(nc, ident[:])
 
@@ -79,6 +84,9 @@ def tile_neuralobliviousdecisiontree_t_kernel(tc, x, W, b, leaf_values, out):
         nc.sync.dma_start(out=bt[0:DEPTH, TREES : 2 * TREES], in_=b)
         load_x(0)
         load_x(1)
+        lr = const.tile([P, LEAVES, DOUT], BF16, name="lr")
+        nc.sync.dma_start(out=lr[0:TREES], in_=leaf_values)
+        nc.sync.dma_start(out=lr[TREES : 2 * TREES], in_=leaf_values)
         load_x(2)
 
         wg = const.tile([P, 2, DEPTH, P, 4], BF16, name="wg", align_bytes=64)
@@ -189,28 +197,61 @@ def tile_neuralobliviousdecisiontree_t_kernel(tc, x, W, b, leaf_values, out):
                     )
             q_t[k] = q
 
-        def products(k):
+        def factors(k):
             q = q_t[k]
             at = ab_pool.tile([P, 2, 2, NB], F32, name="at")
             bb = ab_pool.tile([P, NB, 2, 2], F32, name="bb")
-            nc.vector.tensor_tensor(
+            eng_a = nc.gpsimd if A_ON_G else nc.vector
+            eng_b = nc.gpsimd if B_ON_G else nc.vector
+            eng_a.tensor_tensor(
                 out=at[:],
                 in0=q[:, 0].unsqueeze(2).to_broadcast([P, 2, 2, NB]),
                 in1=q[:, 1].unsqueeze(1).to_broadcast([P, 2, 2, NB]),
                 op=ALU.mult,
             )
-            nc.vector.tensor_tensor(
+            eng_b.tensor_tensor(
                 out=bb[:],
                 in0=q[:, 2].rearrange("p s n -> p n s").unsqueeze(3).to_broadcast([P, NB, 2, 2]),
                 in1=q[:, 3].rearrange("p s n -> p n s").unsqueeze(2).to_broadcast([P, NB, 2, 2]),
                 op=ALU.mult,
             )
+            f_t[k] = (at, bb)
+
+        def flip_out(k):
+            at = f_t[k][0]
+            an = an_pool.tile([P, R, 4, P], F32, name="an")
+            for r in PSUM_R:
+                t1 = ps_x.tile([P, 4, P], F32, name="t1", tag="xt")
+                for a in range(4):
+                    nc.tensor.transpose(
+                        t1[:, a, :],
+                        at[:].rearrange("p s c n -> p (s c) n")[:, a, r * P : (r + 1) * P],
+                        ident[:],
+                    )
+                nc.scalar.copy(out=an[:, r], in_=t1[:])
+            an_t[k] = an
+
+        def flip_back(k):
+            an = an_t[k]
+            a2_t[k] = {}
+            for r in PSUM_R:
+                a2 = ps_a.tile([P, 4, P], F32, name="a2")
+                for a in range(4):
+                    nc.tensor.transpose(a2[:, a, :], an[:, r, a, :], ident[:])
+                a2_t[k][r] = a2
+
+        def products(k):
+            at, bb = f_t[k]
             pa = pa_pool.tile([P, R, 4, P, 4], BF16, name="pa", align_bytes=64)
             for r in range(R):
                 cols = slice(r * P, (r + 1) * P)
+                if r in PSUM_R:
+                    first = a2_t[k][r][:]
+                else:
+                    first = at[:].rearrange("p s c n -> p (s c) n")[:, :, cols]
                 nc.vector.tensor_tensor(
                     out=pa[:, r],
-                    in0=at[:].rearrange("p s c n -> p (s c) n")[:, :, cols].unsqueeze(3).to_broadcast([P, 4, P, 4]),
+                    in0=first.unsqueeze(3).to_broadcast([P, 4, P, 4]),
                     in1=bb[:].rearrange("p n s c -> p n (s c)")[:, cols, :].unsqueeze(1).to_broadcast([P, 4, P, 4]),
                     op=ALU.mult,
                 )
@@ -256,19 +297,25 @@ def tile_neuralobliviousdecisiontree_t_kernel(tc, x, W, b, leaf_values, out):
                     )
 
         units = []
-        for k in range(-3, NBLK + 1):
-            if 3 <= k + 6 < NBLK:
-                load_x(k + 6)
-            if 0 <= k + 1 < NBLK:
-                stage1(k + 1)
+        for k in range(-6, NBLK + 1):
+            if 3 <= k + 9 < NBLK:
+                load_x(k + 9)
+            if 0 <= k + 4 < NBLK:
+                stage1(k + 4)
+            if 0 <= k + 3 < NBLK:
+                factors(k + 3)
+            if 0 <= k + 2 < NBLK:
+                flip_out(k + 2)
             if 0 <= k < 2:
                 leaf_regroup(2 * k)
                 leaf_regroup(2 * k + 1)
             if 0 <= k < NBLK:
                 products(k)
                 quant_path(k, 0)
-            if 0 <= k + 2 < NBLK:
-                quant_x(k + 2)
+            if 0 <= k + 1 < NBLK:
+                flip_back(k + 1)
+            if 0 <= k + 5 < NBLK:
+                quant_x(k + 5)
             if 0 <= k < NBLK:
                 quant_path(k, 1)
             if k == LEAF_AT:
@@ -281,6 +328,6 @@ def tile_neuralobliviousdecisiontree_t_kernel(tc, x, W, b, leaf_values, out):
                 for kk, r in units[:3]:
                     stage2(kk, r)
                 units = units[3:]
-            if 0 <= k + 3 < NBLK:
-                transpose_x(k + 3)
+            if 0 <= k + 6 < NBLK:
+                transpose_x(k + 6)
         assert len(units) == 0

@@ -25,9 +25,6 @@ R = NB // P
 NBLK = HALF // NB
 PIN = False
 LEAF_AT = 2
-PSUM_R = (0, 1)
-A_ON_G = True
-B_ON_G = True
 
 FLOPS = 2 * ROWS * FEAT * DEPTH * TREES + 2 * ROWS * TREES * LEAVES * DOUT
 
@@ -42,8 +39,8 @@ def tile_neuralobliviousdecisiontree_t_kernel(tc, x, W, b, leaf_values, out):
         gx_pool = ctx.enter_context(tc.tile_pool(name="gx", bufs=2))
         cx_pool = ctx.enter_context(tc.tile_pool(name="cx", bufs=2))
         q_pool = ctx.enter_context(tc.tile_pool(name="q", bufs=2))
-        ab_pool = ctx.enter_context(tc.tile_pool(name="ab", bufs=4))
         an_pool = ctx.enter_context(tc.tile_pool(name="an", bufs=2))
+        bb_pool = ctx.enter_context(tc.tile_pool(name="bb", bufs=4))
         pa_pool = ctx.enter_context(tc.tile_pool(name="pa", bufs=2))
         pc_pool = ctx.enter_context(tc.tile_pool(name="pc", bufs=4))
         o_pool = ctx.enter_context(tc.tile_pool(name="o", bufs=4))
@@ -58,12 +55,11 @@ def tile_neuralobliviousdecisiontree_t_kernel(tc, x, W, b, leaf_values, out):
         gx_t = {}
         cx_t = {}
         q_t = {}
-        ab_t = {}
+        f_t = {}
+        a2_t = {}
+        pa_t = {}
         pc_t = {}
         o_t = {}
-        f_t = {}
-        an_t = {}
-        a2_t = {}
 
         def load_x(k):
             xr = xr_pool.tile([P, 2, R * FEAT], BF16, name="xr")
@@ -78,36 +74,51 @@ def tile_neuralobliviousdecisiontree_t_kernel(tc, x, W, b, leaf_values, out):
             out=wr[:].rearrange("q j (u e) t -> q (j u) (e t)", u=2, e=2),
             in_=W.rearrange("j (u q e) t -> q (j u) (e t)", u=2, q=P, e=2),
         )
+        load_x(0)
         bt = const.tile([P, P], BF16, name="bt")
         nc.vector.memset(bt[:], 0.0)
         nc.sync.dma_start(out=bt[0:DEPTH, 0:TREES], in_=b)
         nc.sync.dma_start(out=bt[0:DEPTH, TREES : 2 * TREES], in_=b)
-        load_x(0)
+        b01 = const.tile([P, 2 * TREES], BF16, name="b01")
+        nc.sync.dma_start(
+            out=b01[:], in_=b[0:2, :].rearrange("j t -> (j t)").partition_broadcast(P)
+        )
         load_x(1)
         lr = const.tile([P, LEAVES, DOUT], BF16, name="lr")
         nc.sync.dma_start(out=lr[0:TREES], in_=leaf_values)
         nc.sync.dma_start(out=lr[TREES : 2 * TREES], in_=leaf_values)
         load_x(2)
 
-        wg = const.tile([P, 2, DEPTH, P, 4], BF16, name="wg", align_bytes=64)
+        wg = const.tile([P, 2, 2, P, 4], BF16, name="wg", align_bytes=64)
         nc.vector.memset(wg[:].rearrange("q v j m c -> q (v j m c)").bitcast(I32), 0)
         lc = const.tile([P, 2, 4, DOUT], U32, name="lc", align_bytes=64)
         ls = const.tile([P, 4, DOUT], U8, name="ls", align_bytes=64)
         nc.vector.memset(lc[0:TREES, 1].bitcast(I32), 0)
 
+        wgn = const.tile([P, 2, TREES, 4], BF16, name="wgn", align_bytes=64)
+        nc.vector.tensor_copy(out=wgn[:], in_=wr[:, 0:2].rearrange("q j c t -> q j t c"))
         for v in range(2):
             nc.vector.tensor_copy(
                 out=wg[:, v, :, v * TREES : (v + 1) * TREES, :],
-                in_=wr[:].rearrange("q j c t -> q j t c"),
+                in_=wr[:, 2:4].rearrange("q j c t -> q j t c"),
             )
-        wc = const.tile([P, 2 * DEPTH * P], U32, name="wc", align_bytes=64)
-        ws = const.tile([P, 2 * DEPTH * P], U8, name="ws", align_bytes=64)
+        wcn = const.tile([P, 2 * TREES], U32, name="wcn", align_bytes=64)
+        wsn = const.tile([P, 2 * TREES], U8, name="wsn", align_bytes=64)
+        nc.vector.quantize_mx(
+            out=wcn[:].bitcast(FP8X4),
+            scales=wsn[:],
+            in_=wgn[:].rearrange("q j t c -> q (j t c)"),
+        )
+        wc = const.tile([P, 4 * P], U32, name="wc", align_bytes=64)
+        ws = const.tile([P, 4 * P], U8, name="ws", align_bytes=64)
         nc.vector.quantize_mx(
             out=wc[:].bitcast(FP8X4),
             scales=ws[:],
             in_=wg[:].rearrange("q v j m c -> q (v j m c)"),
         )
 
+        bbc = const.tile([P, 2, TREES], F32, name="bbc")
+        nc.vector.tensor_copy(out=bbc[:].rearrange("p j t -> p (j t)"), in_=b01[:])
         btf = const.tile([P, P], F32, name="btf")
         nc.vector.tensor_copy(out=btf[:], in_=bt[:])
         pb = ps_x.tile([P, P], F32, name="pb", tag="xt")
@@ -169,99 +180,108 @@ def tile_neuralobliviousdecisiontree_t_kernel(tc, x, W, b, leaf_values, out):
 
         def stage1(k):
             cx, sx = cx_t[k]
-            q = q_pool.tile([P, DEPTH, 2, NB], F32, name="q")
-            for jp in range(DEPTH // 2):
-                z = ps_z.tile([P, 2, NB], F32, name="z")
-                for jj in range(2):
-                    j = 2 * jp + jj
-                    for v in range(2):
-                        w0 = (v * DEPTH + j) * P
-                        nc.tensor.matmul_mx(
-                            out=z[:, jj, :],
-                            lhsT=wc[:, w0 : w0 + P].bitcast(FP8X4),
-                            lhsT_scale=ws[:, w0 : w0 + P],
-                            rhs=cx[:, v, :].bitcast(FP8X4),
-                            rhs_scale=sx[:, v, :],
-                            start=(v == 0),
-                            stop=(v == 1),
-                        )
-                for jj in range(2):
-                    j = 2 * jp + jj
-                    nc.scalar.activation(
-                        out=q[:, j, 0, :], in_=z[:, jj, :], func=ACT.Sigmoid,
-                        bias=bpos[:, j : j + 1], scale=1.0,
+            zn = ps_z.tile([P, 2 * R, 2, TREES], F32, name="zn", tag="z")
+            for r in range(R):
+                for h in range(2):
+                    nc.tensor.matmul_mx(
+                        out=zn[:, 2 * r + h].rearrange("p j t -> p (j t)"),
+                        lhsT=cx[:, h, r * P : (r + 1) * P].bitcast(FP8X4),
+                        lhsT_scale=sx[:, h, r * P : (r + 1) * P],
+                        rhs=wcn[:].bitcast(FP8X4),
+                        rhs_scale=wsn[:],
+                        start=True,
+                        stop=True,
                     )
-                    nc.scalar.activation(
-                        out=q[:, j, 1, :], in_=z[:, jj, :], func=ACT.Sigmoid,
-                        bias=bneg[:, j : j + 1], scale=-1.0,
+            zk = ps_z.tile([P, 2, NB], F32, name="zk", tag="z")
+            for jj in range(2):
+                for v in range(2):
+                    w0 = (v * 2 + jj) * P
+                    nc.tensor.matmul_mx(
+                        out=zk[:, jj, :],
+                        lhsT=wc[:, w0 : w0 + P].bitcast(FP8X4),
+                        lhsT_scale=ws[:, w0 : w0 + P],
+                        rhs=cx[:, v, :].bitcast(FP8X4),
+                        rhs_scale=sx[:, v, :],
+                        start=(v == 0),
+                        stop=(v == 1),
                     )
-            q_t[k] = q
+            zb = q_pool.tile([P, 2, 2 * R, TREES], F32, name="zb")
+            nc.vector.tensor_tensor(
+                out=zb[:],
+                in0=zn[:].rearrange("p g j t -> p j g t"),
+                in1=bbc[:].unsqueeze(2).to_broadcast([P, 2, 2 * R, TREES]),
+                op=ALU.add,
+            )
+            qn = q_pool.tile([P, 2, 2, 2 * R * TREES], F32, name="qn")
+            for s in range(2):
+                nc.scalar.activation(
+                    out=qn[:, s].rearrange("p j c -> p (j c)"),
+                    in_=zb[:].rearrange("p j g t -> p (j g t)"),
+                    func=ACT.Sigmoid,
+                    scale=1.0 - 2.0 * s,
+                )
+            qk = q_pool.tile([P, 2, 2, NB], F32, name="qk")
+            for jj in range(2):
+                j = 2 + jj
+                nc.scalar.activation(
+                    out=qk[:, jj, 0, :], in_=zk[:, jj, :], func=ACT.Sigmoid,
+                    bias=bpos[:, j : j + 1], scale=1.0,
+                )
+                nc.scalar.activation(
+                    out=qk[:, jj, 1, :], in_=zk[:, jj, :], func=ACT.Sigmoid,
+                    bias=bneg[:, j : j + 1], scale=-1.0,
+                )
+            q_t[k] = (qn, qk)
 
         def factors(k):
-            q = q_t[k]
-            at = ab_pool.tile([P, 2, 2, NB], F32, name="at")
-            bb = ab_pool.tile([P, NB, 2, 2], F32, name="bb")
-            eng_a = nc.gpsimd if A_ON_G else nc.vector
-            eng_b = nc.gpsimd if B_ON_G else nc.vector
-            eng_a.tensor_tensor(
-                out=at[:],
-                in0=q[:, 0].unsqueeze(2).to_broadcast([P, 2, 2, NB]),
-                in1=q[:, 1].unsqueeze(1).to_broadcast([P, 2, 2, NB]),
+            qn, qk = q_t[k]
+            an = an_pool.tile([P, 2, 2, 2 * R * TREES], F32, name="an")
+            bb = bb_pool.tile([P, NB, 2, 2], F32, name="bb")
+            nc.gpsimd.tensor_tensor(
+                out=an[:],
+                in0=qn[:, :, 0, :].unsqueeze(2).to_broadcast([P, 2, 2, 2 * R * TREES]),
+                in1=qn[:, :, 1, :].unsqueeze(1).to_broadcast([P, 2, 2, 2 * R * TREES]),
                 op=ALU.mult,
             )
-            eng_b.tensor_tensor(
+            nc.gpsimd.tensor_tensor(
                 out=bb[:],
-                in0=q[:, 2].rearrange("p s n -> p n s").unsqueeze(3).to_broadcast([P, NB, 2, 2]),
-                in1=q[:, 3].rearrange("p s n -> p n s").unsqueeze(2).to_broadcast([P, NB, 2, 2]),
+                in0=qk[:, 0].rearrange("p s n -> p n s").unsqueeze(3).to_broadcast([P, NB, 2, 2]),
+                in1=qk[:, 1].rearrange("p s n -> p n s").unsqueeze(2).to_broadcast([P, NB, 2, 2]),
                 op=ALU.mult,
             )
-            f_t[k] = (at, bb)
+            f_t[k] = (an, bb)
 
-        def flip_out(k):
-            at = f_t[k][0]
-            an = an_pool.tile([P, R, 4, P], F32, name="an")
-            for r in PSUM_R:
-                t1 = ps_x.tile([P, 4, P], F32, name="t1", tag="xt")
-                for a in range(4):
-                    nc.tensor.transpose(
-                        t1[:, a, :],
-                        at[:].rearrange("p s c n -> p (s c) n")[:, a, r * P : (r + 1) * P],
-                        ident[:],
-                    )
-                nc.scalar.copy(out=an[:, r], in_=t1[:])
-            an_t[k] = an
-
-        def flip_back(k):
-            an = an_t[k]
-            a2_t[k] = {}
-            for r in PSUM_R:
+        def flip(k):
+            an = f_t[k][0]
+            a2_t[k] = []
+            for r in range(R):
                 a2 = ps_a.tile([P, 4, P], F32, name="a2")
                 for a in range(4):
-                    nc.tensor.transpose(a2[:, a, :], an[:, r, a, :], ident[:])
-                a2_t[k][r] = a2
+                    nc.tensor.transpose(
+                        a2[:, a, :],
+                        an[:].rearrange("p s c n -> p (s c) n")[:, a, r * P : (r + 1) * P],
+                        ident[:],
+                    )
+                a2_t[k].append(a2)
 
         def products(k):
-            at, bb = f_t[k]
+            bb = f_t[k][1]
             pa = pa_pool.tile([P, R, 4, P, 4], BF16, name="pa", align_bytes=64)
             for r in range(R):
-                cols = slice(r * P, (r + 1) * P)
-                if r in PSUM_R:
-                    first = a2_t[k][r][:]
-                else:
-                    first = at[:].rearrange("p s c n -> p (s c) n")[:, :, cols]
                 nc.vector.tensor_tensor(
                     out=pa[:, r],
-                    in0=first.unsqueeze(3).to_broadcast([P, 4, P, 4]),
-                    in1=bb[:].rearrange("p n s c -> p n (s c)")[:, cols, :].unsqueeze(1).to_broadcast([P, 4, P, 4]),
+                    in0=a2_t[k][r][:].unsqueeze(3).to_broadcast([P, 4, P, 4]),
+                    in1=bb[:].rearrange("p n s c -> p n (s c)")[:, r * P : (r + 1) * P, :]
+                    .unsqueeze(1).to_broadcast([P, 4, P, 4]),
                     op=ALU.mult,
                 )
             pc = pc_pool.tile([P, R, 4, P], U32, name="pc", align_bytes=64)
             ps = pc_pool.tile([P, R, 4, P], U8, name="ps", align_bytes=64)
-            ab_t[k] = pa
+            pa_t[k] = pa
             pc_t[k] = (pc, ps)
 
         def quant_path(k, r):
-            pa = ab_t[k]
+            pa = pa_t[k]
             pc, ps = pc_t[k]
             nc.vector.quantize_mx(
                 out=pc[:, r].rearrange("p a n -> p (a n)").bitcast(FP8X4),
@@ -297,15 +317,13 @@ def tile_neuralobliviousdecisiontree_t_kernel(tc, x, W, b, leaf_values, out):
                     )
 
         units = []
-        for k in range(-6, NBLK + 1):
-            if 3 <= k + 9 < NBLK:
-                load_x(k + 9)
-            if 0 <= k + 4 < NBLK:
-                stage1(k + 4)
+        for k in range(-5, NBLK + 1):
+            if 3 <= k + 8 < NBLK:
+                load_x(k + 8)
             if 0 <= k + 3 < NBLK:
-                factors(k + 3)
+                stage1(k + 3)
             if 0 <= k + 2 < NBLK:
-                flip_out(k + 2)
+                factors(k + 2)
             if 0 <= k < 2:
                 leaf_regroup(2 * k)
                 leaf_regroup(2 * k + 1)
@@ -313,9 +331,9 @@ def tile_neuralobliviousdecisiontree_t_kernel(tc, x, W, b, leaf_values, out):
                 products(k)
                 quant_path(k, 0)
             if 0 <= k + 1 < NBLK:
-                flip_back(k + 1)
-            if 0 <= k + 5 < NBLK:
-                quant_x(k + 5)
+                flip(k + 1)
+            if 0 <= k + 4 < NBLK:
+                quant_x(k + 4)
             if 0 <= k < NBLK:
                 quant_path(k, 1)
             if k == LEAF_AT:
@@ -328,6 +346,6 @@ def tile_neuralobliviousdecisiontree_t_kernel(tc, x, W, b, leaf_values, out):
                 for kk, r in units[:3]:
                     stage2(kk, r)
                 units = units[3:]
-            if 0 <= k + 6 < NBLK:
-                transpose_x(k + 6)
+            if 0 <= k + 5 < NBLK:
+                transpose_x(k + 5)
         assert len(units) == 0

@@ -23,8 +23,7 @@ HALF = ROWS // 2
 NB = 256
 R = NB // P
 NBLK = HALF // NB
-PIN = False
-LEAF_AT = 2
+PIN = True
 
 FLOPS = 2 * ROWS * FEAT * DEPTH * TREES + 2 * ROWS * TREES * LEAVES * DOUT
 
@@ -40,9 +39,9 @@ def tile_neuralobliviousdecisiontree_t_kernel(tc, x, W, b, leaf_values, out):
         cx_pool = ctx.enter_context(tc.tile_pool(name="cx", bufs=2))
         q_pool = ctx.enter_context(tc.tile_pool(name="q", bufs=2))
         an_pool = ctx.enter_context(tc.tile_pool(name="an", bufs=2))
-        bb_pool = ctx.enter_context(tc.tile_pool(name="bb", bufs=4))
+        bb_pool = ctx.enter_context(tc.tile_pool(name="bb", bufs=2))
         pa_pool = ctx.enter_context(tc.tile_pool(name="pa", bufs=2))
-        pc_pool = ctx.enter_context(tc.tile_pool(name="pc", bufs=4))
+        pc_pool = ctx.enter_context(tc.tile_pool(name="pc", bufs=3))
         o_pool = ctx.enter_context(tc.tile_pool(name="o", bufs=4))
         ps_x = ctx.enter_context(tc.psum_pool(name="psx", bufs=2))
         ps_z = ctx.enter_context(tc.psum_pool(name="psz", bufs=2))
@@ -54,7 +53,9 @@ def tile_neuralobliviousdecisiontree_t_kernel(tc, x, W, b, leaf_values, out):
         xr_t = {}
         gx_t = {}
         cx_t = {}
-        q_t = {}
+        z_t = {}
+        qn_t = {}
+        qk_t = {}
         f_t = {}
         a2_t = {}
         pa_t = {}
@@ -75,6 +76,7 @@ def tile_neuralobliviousdecisiontree_t_kernel(tc, x, W, b, leaf_values, out):
             in_=W.rearrange("j (u q e) t -> q (j u) (e t)", u=2, q=P, e=2),
         )
         load_x(0)
+        load_x(1)
         bt = const.tile([P, P], BF16, name="bt")
         nc.vector.memset(bt[:], 0.0)
         nc.sync.dma_start(out=bt[0:DEPTH, 0:TREES], in_=b)
@@ -83,7 +85,6 @@ def tile_neuralobliviousdecisiontree_t_kernel(tc, x, W, b, leaf_values, out):
         nc.sync.dma_start(
             out=b01[:], in_=b[0:2, :].rearrange("j t -> (j t)").partition_broadcast(P)
         )
-        load_x(1)
         lr = const.tile([P, LEAVES, DOUT], BF16, name="lr")
         nc.sync.dma_start(out=lr[0:TREES], in_=leaf_values)
         nc.sync.dma_start(out=lr[TREES : 2 * TREES], in_=leaf_values)
@@ -133,10 +134,12 @@ def tile_neuralobliviousdecisiontree_t_kernel(tc, x, W, b, leaf_values, out):
         lg = const.tile([P, 4, DOUT, 4], BF16, name="lg", align_bytes=64)
 
         def leaf_regroup(a):
-            nc.scalar.copy(
-                out=lg[:, a].rearrange("p (c i) t -> p c t i", i=4),
-                in_=lr[:, 4 * a : 4 * a + 4, :].rearrange("p t (c i) -> p c t i", i=4),
-            )
+            dst = lg[:, a].rearrange("p (c i) t -> p c t i", i=4)
+            src = lr[:, 4 * a : 4 * a + 4, :].rearrange("p t (c i) -> p c t i", i=4)
+            if a < 2:
+                nc.vector.tensor_copy(out=dst, in_=src)
+            else:
+                nc.scalar.copy(out=dst, in_=src)
 
         def leaf_quant():
             for g in range(2):
@@ -178,7 +181,7 @@ def tile_neuralobliviousdecisiontree_t_kernel(tc, x, W, b, leaf_values, out):
             )
             cx_t[k] = (cx, sx)
 
-        def stage1(k):
+        def stage1_pe(k):
             cx, sx = cx_t[k]
             zn = ps_z.tile([P, 2 * R, 2, TREES], F32, name="zn", tag="z")
             for r in range(R):
@@ -205,6 +208,10 @@ def tile_neuralobliviousdecisiontree_t_kernel(tc, x, W, b, leaf_values, out):
                         start=(v == 0),
                         stop=(v == 1),
                     )
+            z_t[k] = (zn, zk)
+
+        def bias_rows(k):
+            zn = z_t[k][0]
             zb = q_pool.tile([P, 2, 2 * R, TREES], F32, name="zb")
             nc.vector.tensor_tensor(
                 out=zb[:],
@@ -220,6 +227,10 @@ def tile_neuralobliviousdecisiontree_t_kernel(tc, x, W, b, leaf_values, out):
                     func=ACT.Sigmoid,
                     scale=1.0 - 2.0 * s,
                 )
+            qn_t[k] = qn
+
+        def sigmoid_cols(k):
+            zk = z_t[k][1]
             qk = q_pool.tile([P, 2, 2, NB], F32, name="qk")
             for jj in range(2):
                 j = 2 + jj
@@ -231,10 +242,11 @@ def tile_neuralobliviousdecisiontree_t_kernel(tc, x, W, b, leaf_values, out):
                     out=qk[:, jj, 1, :], in_=zk[:, jj, :], func=ACT.Sigmoid,
                     bias=bneg[:, j : j + 1], scale=-1.0,
                 )
-            q_t[k] = (qn, qk)
+            qk_t[k] = qk
 
         def factors(k):
-            qn, qk = q_t[k]
+            qn = qn_t[k]
+            qk = qk_t[k]
             an = an_pool.tile([P, 2, 2, 2 * R * TREES], F32, name="an")
             bb = bb_pool.tile([P, NB, 2, 2], F32, name="bb")
             nc.gpsimd.tensor_tensor(
@@ -251,34 +263,31 @@ def tile_neuralobliviousdecisiontree_t_kernel(tc, x, W, b, leaf_values, out):
             )
             f_t[k] = (an, bb)
 
-        def flip(k):
+        def flip(k, r):
             an = f_t[k][0]
-            a2_t[k] = []
-            for r in range(R):
-                a2 = ps_a.tile([P, 4, P], F32, name="a2")
-                for a in range(4):
-                    nc.tensor.transpose(
-                        a2[:, a, :],
-                        an[:].rearrange("p s c n -> p (s c) n")[:, a, r * P : (r + 1) * P],
-                        ident[:],
-                    )
-                a2_t[k].append(a2)
-
-        def products(k):
-            bb = f_t[k][1]
-            pa = pa_pool.tile([P, R, 4, P, 4], BF16, name="pa", align_bytes=64)
-            for r in range(R):
-                nc.vector.tensor_tensor(
-                    out=pa[:, r],
-                    in0=a2_t[k][r][:].unsqueeze(3).to_broadcast([P, 4, P, 4]),
-                    in1=bb[:].rearrange("p n s c -> p n (s c)")[:, r * P : (r + 1) * P, :]
-                    .unsqueeze(1).to_broadcast([P, 4, P, 4]),
-                    op=ALU.mult,
+            a2 = ps_a.tile([P, 4, P], F32, name="a2")
+            for a in range(4):
+                nc.tensor.transpose(
+                    a2[:, a, :],
+                    an[:].rearrange("p s c n -> p (s c) n")[:, a, r * P : (r + 1) * P],
+                    ident[:],
                 )
-            pc = pc_pool.tile([P, R, 4, P], U32, name="pc", align_bytes=64)
-            ps = pc_pool.tile([P, R, 4, P], U8, name="ps", align_bytes=64)
-            pa_t[k] = pa
-            pc_t[k] = (pc, ps)
+            a2_t[(k, r)] = a2
+
+        def product(k, r):
+            bb = f_t[k][1]
+            if r == 0:
+                pa_t[k] = pa_pool.tile([P, R, 4, P, 4], BF16, name="pa", align_bytes=64)
+                pc = pc_pool.tile([P, R, 4, P], U32, name="pc", align_bytes=64)
+                ps = pc_pool.tile([P, R, 4, P], U8, name="ps", align_bytes=64)
+                pc_t[k] = (pc, ps)
+            nc.vector.tensor_tensor(
+                out=pa_t[k][:, r],
+                in0=a2_t[(k, r)][:].unsqueeze(3).to_broadcast([P, 4, P, 4]),
+                in1=bb[:].rearrange("p n s c -> p n (s c)")[:, r * P : (r + 1) * P, :]
+                .unsqueeze(1).to_broadcast([P, 4, P, 4]),
+                op=ALU.mult,
+            )
 
         def quant_path(k, r):
             pa = pa_t[k]
@@ -316,36 +325,42 @@ def tile_neuralobliviousdecisiontree_t_kernel(tc, x, W, b, leaf_values, out):
                         in_=o[:],
                     )
 
-        units = []
-        for k in range(-5, NBLK + 1):
-            if 3 <= k + 8 < NBLK:
-                load_x(k + 8)
-            if 0 <= k + 3 < NBLK:
-                stage1(k + 3)
-            if 0 <= k + 2 < NBLK:
-                factors(k + 2)
-            if 0 <= k < 2:
-                leaf_regroup(2 * k)
-                leaf_regroup(2 * k + 1)
-            if 0 <= k < NBLK:
-                products(k)
-                quant_path(k, 0)
-            if 0 <= k + 1 < NBLK:
-                flip(k + 1)
-            if 0 <= k + 4 < NBLK:
-                quant_x(k + 4)
-            if 0 <= k < NBLK:
-                quant_path(k, 1)
-            if k == LEAF_AT:
+        def live(k):
+            return 0 <= k < NBLK
+
+        last = NBLK - 1
+        for i in range(-3, NBLK + 1):
+            if 3 <= i + 6 < NBLK:
+                load_x(i + 6)
+            if live(i + 1):
+                bias_rows(i + 1)
+            if live(i):
+                flip(i, 1)
+            if live(i + 3):
+                transpose_x(i + 3)
+            if live(i + 2):
+                quant_x(i + 2)
+                stage1_pe(i + 2)
+                sigmoid_cols(i + 2)
+            if i == 1:
                 leaf_quant()
-            if 0 <= k - 1 < NBLK:
-                units.append((k - 1, 1))
-            if 0 <= k < NBLK:
-                units.append((k, 0))
-            if k >= LEAF_AT:
-                for kk, r in units[:3]:
-                    stage2(kk, r)
-                units = units[3:]
-            if 0 <= k + 5 < NBLK:
-                transpose_x(k + 5)
-        assert len(units) == 0
+            if live(i - 1) and i - 1 != last:
+                quant_path(i - 1, 0)
+                quant_path(i - 1, 1)
+            if live(i + 1):
+                factors(i + 1)
+            if i == 0:
+                for a in range(4):
+                    leaf_regroup(a)
+            if live(i):
+                product(i, 0)
+                if i == last:
+                    quant_path(i, 0)
+                product(i, 1)
+                if i == last:
+                    quant_path(i, 1)
+            if live(i - 1):
+                stage2(i - 1, 0)
+                stage2(i - 1, 1)
+            if live(i + 1):
+                flip(i + 1, 0)

@@ -83,7 +83,7 @@ def tile_neuralobliviousdecisiontree_t_kernel(tc, x, W, b, leaf_values, out):
         nc.sync.dma_start(out=bt[0:DEPTH, TREES : 2 * TREES], in_=b)
         b01 = const.tile([P, 2 * TREES], BF16, name="b01")
         nc.sync.dma_start(
-            out=b01[:], in_=b[0:2, :].rearrange("j t -> (j t)").partition_broadcast(P)
+            out=b01[:], in_=b[2:4, :].rearrange("j t -> (j t)").partition_broadcast(P)
         )
         lr = const.tile([P, LEAVES, DOUT], BF16, name="lr")
         nc.sync.dma_start(out=lr[0:TREES], in_=leaf_values)
@@ -97,11 +97,11 @@ def tile_neuralobliviousdecisiontree_t_kernel(tc, x, W, b, leaf_values, out):
         nc.vector.memset(lc[0:TREES, 1].bitcast(I32), 0)
 
         wgn = const.tile([P, 2, TREES, 4], BF16, name="wgn", align_bytes=64)
-        nc.vector.tensor_copy(out=wgn[:], in_=wr[:, 0:2].rearrange("q j c t -> q j t c"))
+        nc.vector.tensor_copy(out=wgn[:], in_=wr[:, 2:4].rearrange("q j c t -> q j t c"))
         for v in range(2):
             nc.vector.tensor_copy(
                 out=wg[:, v, :, v * TREES : (v + 1) * TREES, :],
-                in_=wr[:, 2:4].rearrange("q j c t -> q j t c"),
+                in_=wr[:, 0:2].rearrange("q j c t -> q j t c"),
             )
         wcn = const.tile([P, 2 * TREES], U32, name="wcn", align_bytes=64)
         wsn = const.tile([P, 2 * TREES], U8, name="wsn", align_bytes=64)
@@ -233,7 +233,7 @@ def tile_neuralobliviousdecisiontree_t_kernel(tc, x, W, b, leaf_values, out):
             zk = z_t[k][1]
             qk = q_pool.tile([P, 2, 2, NB], F32, name="qk")
             for jj in range(2):
-                j = 2 + jj
+                j = jj
                 nc.scalar.activation(
                     out=qk[:, jj, 0, :], in_=zk[:, jj, :], func=ACT.Sigmoid,
                     bias=bpos[:, j : j + 1], scale=1.0,
@@ -248,7 +248,7 @@ def tile_neuralobliviousdecisiontree_t_kernel(tc, x, W, b, leaf_values, out):
             qn = qn_t[k]
             qk = qk_t[k]
             an = an_pool.tile([P, 2, 2, 2 * R * TREES], F32, name="an")
-            bb = bb_pool.tile([P, NB, 2, 2], F32, name="bb")
+            bb = bb_pool.tile([P, 2, 2, NB], F32, name="bb")
             nc.gpsimd.tensor_tensor(
                 out=an[:],
                 in0=qn[:, :, 0, :].unsqueeze(2).to_broadcast([P, 2, 2, 2 * R * TREES]),
@@ -257,8 +257,8 @@ def tile_neuralobliviousdecisiontree_t_kernel(tc, x, W, b, leaf_values, out):
             )
             nc.gpsimd.tensor_tensor(
                 out=bb[:],
-                in0=qk[:, 0].rearrange("p s n -> p n s").unsqueeze(3).to_broadcast([P, NB, 2, 2]),
-                in1=qk[:, 1].rearrange("p s n -> p n s").unsqueeze(2).to_broadcast([P, NB, 2, 2]),
+                in0=qk[:, 0].unsqueeze(2).to_broadcast([P, 2, 2, NB]),
+                in1=qk[:, 1].unsqueeze(1).to_broadcast([P, 2, 2, NB]),
                 op=ALU.mult,
             )
             f_t[k] = (an, bb)
@@ -283,9 +283,9 @@ def tile_neuralobliviousdecisiontree_t_kernel(tc, x, W, b, leaf_values, out):
                 pc_t[k] = (pc, ps)
             nc.vector.tensor_tensor(
                 out=pa_t[k][:, r],
-                in0=a2_t[(k, r)][:].unsqueeze(3).to_broadcast([P, 4, P, 4]),
-                in1=bb[:].rearrange("p n s c -> p n (s c)")[:, r * P : (r + 1) * P, :]
-                .unsqueeze(1).to_broadcast([P, 4, P, 4]),
+                in0=a2_t[(k, r)][:].rearrange("p i n -> p n i").unsqueeze(1).to_broadcast([P, 4, P, 4]),
+                in1=bb[:].rearrange("p s c n -> p (s c) n")[:, :, r * P : (r + 1) * P]
+                .unsqueeze(3).to_broadcast([P, 4, P, 4]),
                 op=ALU.mult,
             )
 

@@ -263,6 +263,9 @@ def tile_neuralobliviousdecisiontree_t_kernel(tc, x, W, b, leaf_values, out):
             )
             f_t[k] = (an, bb)
 
+        def hold_gpsimd(k):
+            nc.gpsimd.memset(pa_t[k][:, R - 1, 3, P - 1, 2:4], 0.0)
+
         def flip(k, r):
             an = f_t[k][0]
             a2 = ps_a.tile([P, 4, P], F32, name="a2")
@@ -347,6 +350,8 @@ def tile_neuralobliviousdecisiontree_t_kernel(tc, x, W, b, leaf_values, out):
             if live(i - 1) and i - 1 != last:
                 quant_path(i - 1, 0)
                 quant_path(i - 1, 1)
+            if live(i - 1) and live(i + 1):
+                hold_gpsimd(i - 1)
             if live(i + 1):
                 factors(i + 1)
             if i == 0:

@@ -22,6 +22,9 @@ DOUT = 512
 HALF = ROWS // 2
 NB = 256
 R = NB // P
+CW = 2 * R * P
+GW = CW + CW // 4
+RING = 4
 NBLK = HALF // NB
 PIN = True
 
@@ -41,7 +44,6 @@ def tile_neuralobliviousdecisiontree_t_kernel(tc, x, W, b, leaf_values, out):
         an_pool = ctx.enter_context(tc.tile_pool(name="an", bufs=2))
         bb_pool = ctx.enter_context(tc.tile_pool(name="bb", bufs=2))
         pa_pool = ctx.enter_context(tc.tile_pool(name="pa", bufs=2))
-        pc_pool = ctx.enter_context(tc.tile_pool(name="pc", bufs=3))
         o_pool = ctx.enter_context(tc.tile_pool(name="o", bufs=4))
         ps_x = ctx.enter_context(tc.psum_pool(name="psx", bufs=2))
         ps_z = ctx.enter_context(tc.psum_pool(name="psz", bufs=2))
@@ -59,8 +61,6 @@ def tile_neuralobliviousdecisiontree_t_kernel(tc, x, W, b, leaf_values, out):
         f_t = {}
         a2_t = {}
         pa_t = {}
-        pc_t = {}
-        o_t = {}
 
         def load_x(k):
             xr = xr_pool.tile([P, 2, R * FEAT], BF16, name="xr")
@@ -85,16 +85,27 @@ def tile_neuralobliviousdecisiontree_t_kernel(tc, x, W, b, leaf_values, out):
         nc.sync.dma_start(
             out=b01[:], in_=b[2:4, :].rearrange("j t -> (j t)").partition_broadcast(P)
         )
-        lr = const.tile([P, LEAVES, DOUT], BF16, name="lr")
-        nc.sync.dma_start(out=lr[0:TREES], in_=leaf_values)
-        nc.sync.dma_start(out=lr[TREES : 2 * TREES], in_=leaf_values)
+        lr = const.tile([P, LEAVES // 2, DOUT], BF16, name="lr")
+        for u in range(2):
+            nc.sync.dma_start(
+                out=lr[u * TREES : (u + 1) * TREES],
+                in_=leaf_values[:, u * 8 : (u + 1) * 8, :],
+            )
         load_x(2)
 
         wg = const.tile([P, 2, 2, P, 4], BF16, name="wg", align_bytes=64)
         nc.vector.memset(wg[:].rearrange("q v j m c -> q (v j m c)").bitcast(I32), 0)
-        lc = const.tile([P, 2, 4, DOUT], U32, name="lc", align_bytes=64)
-        ls = const.tile([P, 4, DOUT], U8, name="ls", align_bytes=64)
-        nc.vector.memset(lc[0:TREES, 1].bitcast(I32), 0)
+        lc = const.tile([P, 2, DOUT], U32, name="lc", align_bytes=64)
+        ls = const.tile([P, 2, DOUT], U8, name="ls", align_bytes=64)
+        pt_ring = []
+        wt_ring = []
+        for n in range(RING):
+            pt = const.tile([P, 2 * GW], U32, name=f"pt{n}", align_bytes=64)
+            wt = const.tile([P, GW], U32, name=f"wt{n}", align_bytes=64)
+            for g in range(2):
+                nc.gpsimd.memset(pt[:, g * GW + CW : (g + 1) * GW].bitcast(I32), 0)
+            pt_ring.append(pt)
+            wt_ring.append(wt)
 
         wgn = const.tile([P, 2, TREES, 4], BF16, name="wgn", align_bytes=64)
         nc.vector.tensor_copy(out=wgn[:], in_=wr[:, 2:4].rearrange("q j c t -> q j t c"))
@@ -131,28 +142,22 @@ def tile_neuralobliviousdecisiontree_t_kernel(tc, x, W, b, leaf_values, out):
             out=bneg[:], in0=pb[:, 0:DEPTH], scalar1=-1.0, scalar2=None, op0=ALU.mult
         )
 
-        lg = const.tile([P, 4, DOUT, 4], BF16, name="lg", align_bytes=64)
+        lg = const.tile([P, 2, DOUT, 4], BF16, name="lg", align_bytes=64)
 
         def leaf_regroup(a):
             dst = lg[:, a].rearrange("p (c i) t -> p c t i", i=4)
             src = lr[:, 4 * a : 4 * a + 4, :].rearrange("p t (c i) -> p c t i", i=4)
-            if a < 2:
+            if a < 1:
                 nc.vector.tensor_copy(out=dst, in_=src)
             else:
                 nc.scalar.copy(out=dst, in_=src)
 
         def leaf_quant():
-            for g in range(2):
-                nc.vector.quantize_mx(
-                    out=lc[:, 0, 2 * g : 2 * g + 2, :].rearrange("p a d -> p (a d)").bitcast(FP8X4),
-                    scales=ls[:, 2 * g : 2 * g + 2, :].rearrange("p a d -> p (a d)"),
-                    in_=lg[:, 2 * g : 2 * g + 2].rearrange("p a d i -> p (a d i)"),
-                )
-            nc.vector.tensor_copy(
-                out=lc[TREES : 2 * TREES, 1].bitcast(I32),
-                in_=lc[TREES : 2 * TREES, 0].bitcast(I32),
+            nc.vector.quantize_mx(
+                out=lc[:].rearrange("p a d -> p (a d)").bitcast(FP8X4),
+                scales=ls[:].rearrange("p a d -> p (a d)"),
+                in_=lg[:].rearrange("p a d i -> p (a d i)"),
             )
-            nc.vector.memset(lc[TREES : 2 * TREES, 0].bitcast(I32), 0)
 
         def transpose_x(k):
             xr = xr_t[k]
@@ -264,7 +269,7 @@ def tile_neuralobliviousdecisiontree_t_kernel(tc, x, W, b, leaf_values, out):
             f_t[k] = (an, bb)
 
         def hold_gpsimd(k):
-            nc.gpsimd.memset(pa_t[k][:, R - 1, 3, P - 1, 2:4], 0.0)
+            nc.gpsimd.memset(pa_t[k][:, 3, R - 1, P - 1, 2:4], 0.0)
 
         def flip(k, r):
             an = f_t[k][0]
@@ -280,59 +285,62 @@ def tile_neuralobliviousdecisiontree_t_kernel(tc, x, W, b, leaf_values, out):
         def product(k, r):
             bb = f_t[k][1]
             if r == 0:
-                pa_t[k] = pa_pool.tile([P, R, 4, P, 4], BF16, name="pa", align_bytes=64)
-                pc = pc_pool.tile([P, R, 4, P], U32, name="pc", align_bytes=64)
-                ps = pc_pool.tile([P, R, 4, P], U8, name="ps", align_bytes=64)
-                pc_t[k] = (pc, ps)
+                pa_t[k] = pa_pool.tile([P, 4, R, P, 4], BF16, name="pa", align_bytes=64)
             nc.vector.tensor_tensor(
-                out=pa_t[k][:, r],
+                out=pa_t[k][:, :, r],
                 in0=a2_t[(k, r)][:].rearrange("p i n -> p n i").unsqueeze(1).to_broadcast([P, 4, P, 4]),
                 in1=bb[:].rearrange("p s c n -> p (s c) n")[:, :, r * P : (r + 1) * P]
                 .unsqueeze(3).to_broadcast([P, 4, P, 4]),
                 op=ALU.mult,
             )
 
-        def quant_path(k, r):
-            pa = pa_t[k]
-            pc, ps = pc_t[k]
+        def quant_path(k, g):
+            pt = pt_ring[k % RING]
             nc.vector.quantize_mx(
-                out=pc[:, r].rearrange("p a n -> p (a n)").bitcast(FP8X4),
-                scales=ps[:, r].rearrange("p a n -> p (a n)"),
-                in_=pa[:, r].rearrange("p a n i -> p (a n i)"),
+                out=pt[:, g * GW : g * GW + CW].bitcast(FP8X4),
+                scales=pt[:, g * GW + CW : (g + 1) * GW].bitcast(U8),
+                in_=pa_t[k][:, 2 * g : 2 * g + 2].rearrange("p a r n i -> p (a r n i)"),
             )
 
-        def stage2(k, r):
-            pc, ps = pc_t[k]
-            if r == 0:
-                o_t[k] = [o_pool.tile([P, R, DOUT], F32, name="o") for h in range(2)]
-            for h in range(2):
-                o = o_t[k][h]
+        def gather(k):
+            pt = pt_ring[k % RING][:].bitcast(I32)
+            wt = wt_ring[k % RING][:].bitcast(I32)
+            lo = slice(0, TREES)
+            hi = slice(TREES, 2 * TREES)
+            nc.sync.dma_start(out=wt[lo, :], in_=pt[hi, 0:GW])
+            nc.sync.dma_start(out=wt[hi, :], in_=pt[hi, GW : 2 * GW])
+            nc.sync.dma_start(out=pt[hi, 0:GW], in_=pt[lo, GW : 2 * GW])
+
+        def stage2(k, h):
+            src = wt_ring[k % RING] if h == 1 else pt_ring[k % RING]
+            o = o_pool.tile([P, R, DOUT], F32, name="o")
+            for r in range(R):
                 acc = ps_o.tile([P, DOUT], F32, name="acc")
-                for a in range(4):
+                for s in range(2):
+                    c0 = (s * R + r) * P
                     nc.tensor.matmul_mx(
                         out=acc[:],
-                        lhsT=pc[:, r, a, :].bitcast(FP8X4),
-                        lhsT_scale=ps[:, r, a, :],
-                        rhs=lc[:, h, a, :].bitcast(FP8X4),
-                        rhs_scale=ls[:, a, :],
-                        start=(a == 0),
-                        stop=(a == 3),
+                        lhsT=src[:, c0 : c0 + P].bitcast(FP8X4),
+                        lhsT_scale=src[:, CW : GW].bitcast(U8)[:, c0 : c0 + P],
+                        rhs=lc[:, s, :].bitcast(FP8X4),
+                        rhs_scale=ls[:, s, :],
+                        start=(s == 0),
+                        stop=(s == 1),
                     )
                 nc.scalar.activation(
                     out=o[:, r, :], in_=acc[:], func=ACT.Copy, scale=1.0 / TREES
                 )
-                if r == R - 1:
-                    row0 = h * HALF + k * NB
-                    nc.sync.dma_start(
-                        out=out[row0 : row0 + NB, :].rearrange("(p r) d -> p r d", r=R),
-                        in_=o[:],
-                    )
+            row0 = h * HALF + k * NB
+            nc.sync.dma_start(
+                out=out[row0 : row0 + NB, :].rearrange("(p r) d -> p r d", r=R),
+                in_=o[:],
+            )
 
         def live(k):
             return 0 <= k < NBLK
 
         last = NBLK - 1
-        for i in range(-3, NBLK + 1):
+        for i in range(-3, NBLK + 2):
             if 3 <= i + 6 < NBLK:
                 load_x(i + 6)
             if live(i + 1):
@@ -341,6 +349,8 @@ def tile_neuralobliviousdecisiontree_t_kernel(tc, x, W, b, leaf_values, out):
                 flip(i, 1)
             if live(i + 3):
                 transpose_x(i + 3)
+            if live(i - 2):
+                stage2(i - 2, 1)
             if live(i + 2):
                 quant_x(i + 2)
                 stage1_pe(i + 2)
@@ -350,22 +360,22 @@ def tile_neuralobliviousdecisiontree_t_kernel(tc, x, W, b, leaf_values, out):
             if live(i - 1) and i - 1 != last:
                 quant_path(i - 1, 0)
                 quant_path(i - 1, 1)
+                gather(i - 1)
+            if live(i - 2):
+                stage2(i - 2, 0)
             if live(i - 1) and live(i + 1):
                 hold_gpsimd(i - 1)
             if live(i + 1):
                 factors(i + 1)
             if i == 0:
-                for a in range(4):
+                for a in range(2):
                     leaf_regroup(a)
             if live(i):
                 product(i, 0)
-                if i == last:
-                    quant_path(i, 0)
                 product(i, 1)
-                if i == last:
-                    quant_path(i, 1)
-            if live(i - 1):
-                stage2(i - 1, 0)
-                stage2(i - 1, 1)
+            if i == last:
+                quant_path(i, 0)
+                quant_path(i, 1)
+                gather(i)
             if live(i + 1):
                 flip(i + 1, 0)

@@ -273,10 +273,10 @@ def tile_neuralobliviousdecisiontree_t_kernel(tc, x, W, b, leaf_values, out):
 
         def flip(k, r):
             an = f_t[k][0]
-            a2 = ps_a.tile([P, 4, P], F32, name="a2")
+            a2 = ps_a.tile([P, P, 4], F32, name="a2")
             for a in range(4):
                 nc.tensor.transpose(
-                    a2[:, a, :],
+                    a2[:, :, a],
                     an[:].rearrange("p s c n -> p (s c) n")[:, a, r * P : (r + 1) * P],
                     ident[:],
                 )
@@ -288,7 +288,7 @@ def tile_neuralobliviousdecisiontree_t_kernel(tc, x, W, b, leaf_values, out):
                 pa_t[k] = pa_pool.tile([P, 4, R, P, 4], BF16, name="pa", align_bytes=64)
             nc.vector.tensor_tensor(
                 out=pa_t[k][:, :, r],
-                in0=a2_t[(k, r)][:].rearrange("p i n -> p n i").unsqueeze(1).to_broadcast([P, 4, P, 4]),
+                in0=a2_t[(k, r)][:].unsqueeze(1).to_broadcast([P, 4, P, 4]),
                 in1=bb[:].rearrange("p s c n -> p (s c) n")[:, :, r * P : (r + 1) * P]
                 .unsqueeze(3).to_broadcast([P, 4, P, 4]),
                 op=ALU.mult,

@@ -24,7 +24,7 @@ NB = 256
 R = NB // P
 CW = 2 * R * P
 GW = CW + CW // 4
-RING = 4
+RING = 5
 NBLK = HALF // NB
 PIN = True
 
@@ -45,8 +45,8 @@ def tile_neuralobliviousdecisiontree_t_kernel(tc, x, W, b, leaf_values, out):
         bb_pool = ctx.enter_context(tc.tile_pool(name="bb", bufs=2))
         pa_pool = ctx.enter_context(tc.tile_pool(name="pa", bufs=2))
         o_pool = ctx.enter_context(tc.tile_pool(name="o", bufs=4))
-        ps_x = ctx.enter_context(tc.psum_pool(name="psx", bufs=2))
-        ps_z = ctx.enter_context(tc.psum_pool(name="psz", bufs=2))
+        ps_x = ctx.enter_context(tc.psum_pool(name="psx", bufs=1))
+        ps_z = ctx.enter_context(tc.psum_pool(name="psz", bufs=1))
         ps_a = ctx.enter_context(tc.psum_pool(name="psa", bufs=2))
         ps_o = ctx.enter_context(tc.psum_pool(name="pso", bufs=2))
 
@@ -56,6 +56,8 @@ def tile_neuralobliviousdecisiontree_t_kernel(tc, x, W, b, leaf_values, out):
         gx_t = {}
         cx_t = {}
         z_t = {}
+        pr_t = {}
+        zt_t = {}
         qn_t = {}
         qk_t = {}
         f_t = {}
@@ -64,26 +66,29 @@ def tile_neuralobliviousdecisiontree_t_kernel(tc, x, W, b, leaf_values, out):
 
         def load_x(k):
             xr = xr_pool.tile([P, 2, R * FEAT], BF16, name="xr")
-            nc.sync.dma_start(out=xr[:], in_=x_blk[k])
+            if k == 0:
+                for h in range(2):
+                    nc.sync.dma_start(out=xr[:, h], in_=x_blk[k][:, h])
+            else:
+                nc.sync.dma_start(out=xr[:], in_=x_blk[k])
             xr_t[k] = xr
 
         ident = const.tile([P, P], F32, name="ident")
         make_identity(nc, ident[:])
 
         wr = const.tile([P, DEPTH, 4, TREES], BF16, name="wr")
+        bt = const.tile([P, P], BF16, name="bt")
+        nc.gpsimd.memset(bt[:], 0.0)
+        load_x(0)
         nc.sync.dma_start(
             out=wr[:].rearrange("q j (u e) t -> q (j u) (e t)", u=2, e=2),
             in_=W.rearrange("j (u q e) t -> q (j u) (e t)", u=2, q=P, e=2),
         )
-        load_x(0)
         load_x(1)
-        bt = const.tile([P, P], BF16, name="bt")
-        nc.vector.memset(bt[:], 0.0)
-        nc.sync.dma_start(out=bt[0:DEPTH, 0:TREES], in_=b)
-        nc.sync.dma_start(out=bt[0:DEPTH, TREES : 2 * TREES], in_=b)
-        b01 = const.tile([P, 2 * TREES], BF16, name="b01")
+        for n in range(2):
+            nc.sync.dma_start(out=bt[0:DEPTH, n * TREES : (n + 1) * TREES], in_=b)
         nc.sync.dma_start(
-            out=b01[:], in_=b[2:4, :].rearrange("j t -> (j t)").partition_broadcast(P)
+            out=bt[DEPTH : DEPTH + 1, :], in_=b[2:4, :].rearrange("j t -> (j t)").unsqueeze(0)
         )
         lr = const.tile([P, LEAVES // 2, DOUT], BF16, name="lr")
         for u in range(2):
@@ -94,7 +99,7 @@ def tile_neuralobliviousdecisiontree_t_kernel(tc, x, W, b, leaf_values, out):
         load_x(2)
 
         wg = const.tile([P, 2, 2, P, 4], BF16, name="wg", align_bytes=64)
-        nc.vector.memset(wg[:].rearrange("q v j m c -> q (v j m c)").bitcast(I32), 0)
+        nc.gpsimd.memset(wg[:].rearrange("q v j m c -> q (v j m c)").bitcast(I32), 0)
         lc = const.tile([P, 2, DOUT], U32, name="lc", align_bytes=64)
         ls = const.tile([P, 2, DOUT], U8, name="ls", align_bytes=64)
         pt_ring = []
@@ -129,28 +134,25 @@ def tile_neuralobliviousdecisiontree_t_kernel(tc, x, W, b, leaf_values, out):
             in_=wg[:].rearrange("q v j m c -> q (v j m c)"),
         )
 
-        bbc = const.tile([P, 2, TREES], F32, name="bbc")
-        nc.vector.tensor_copy(out=bbc[:].rearrange("p j t -> p (j t)"), in_=b01[:])
-        btf = const.tile([P, P], F32, name="btf")
-        nc.vector.tensor_copy(out=btf[:], in_=bt[:])
-        pb = ps_x.tile([P, P], F32, name="pb", tag="xt")
-        nc.tensor.transpose(pb[:], btf[:], ident[:])
-        bpos = const.tile([P, DEPTH], F32, name="bpos")
-        bneg = const.tile([P, DEPTH], F32, name="bneg")
-        nc.vector.tensor_copy(out=bpos[:], in_=pb[:, 0:DEPTH])
-        nc.vector.tensor_scalar(
-            out=bneg[:], in0=pb[:, 0:DEPTH], scalar1=-1.0, scalar2=None, op0=ALU.mult
-        )
+        bpos = const.tile([P, DEPTH + 1], F32, name="bpos")
+        bneg = const.tile([P, DEPTH + 1], F32, name="bneg")
+
+        def bias_columns():
+            btf = const.tile([P, P], F32, name="btf")
+            nc.vector.tensor_copy(out=btf[:], in_=bt[:])
+            pb = ps_z.tile([P, P], F32, name="pb", tag="zt")
+            nc.tensor.transpose(pb[:], btf[:], ident[:])
+            nc.vector.tensor_copy(out=bpos[:], in_=pb[:, 0 : DEPTH + 1])
+            nc.vector.tensor_scalar(
+                out=bneg[:], in0=pb[:, 0 : DEPTH + 1], scalar1=-1.0, scalar2=None, op0=ALU.mult
+            )
 
         lg = const.tile([P, 2, DOUT, 4], BF16, name="lg", align_bytes=64)
 
         def leaf_regroup(a):
             dst = lg[:, a].rearrange("p (c i) t -> p c t i", i=4)
             src = lr[:, 4 * a : 4 * a + 4, :].rearrange("p t (c i) -> p c t i", i=4)
-            if a < 1:
-                nc.vector.tensor_copy(out=dst, in_=src)
-            else:
-                nc.scalar.copy(out=dst, in_=src)
+            nc.vector.tensor_copy(out=dst, in_=src)
 
         def leaf_quant():
             nc.vector.quantize_mx(
@@ -159,21 +161,21 @@ def tile_neuralobliviousdecisiontree_t_kernel(tc, x, W, b, leaf_values, out):
                 in_=lg[:].rearrange("p a d i -> p (a d i)"),
             )
 
-        def transpose_x(k):
-            xr = xr_t[k]
-            gx = gx_pool.tile([P, 2, NB, 4], BF16, name="gx", align_bytes=64)
-            for h in range(2):
-                xt = ps_x.tile([P, R, 2, P], F32, name="xt", tag="xt")
-                xw = xr[:, h, :].bitcast(F32)
-                for r in range(R):
-                    for u in range(2):
-                        c0 = r * (FEAT // 2) + u * P
-                        nc.tensor.transpose(xt[:, r, u, :], xw[:, c0 : c0 + P], ident[:])
-                nc.scalar.copy(
-                    out=gx[:, h].bitcast(F32).rearrange("q (r p) u -> q r p u", r=R),
-                    in_=xt[:].rearrange("q r u p -> q r p u"),
-                )
-            gx_t[k] = gx
+        last = NBLK - 1
+
+        def transpose_x(k, h):
+            if h == 0:
+                gx_t[k] = gx_pool.tile([P, 2, NB, 4], BF16, name="gx", align_bytes=64)
+            xt = ps_x.tile([P, R, 2, P], F32, name="xt", tag="xt")
+            xw = xr_t[k][:, h, :].bitcast(F32)
+            for r in range(R):
+                for u in range(2):
+                    c0 = r * (FEAT // 2) + u * P
+                    nc.tensor.transpose(xt[:, r, u, :], xw[:, c0 : c0 + P], ident[:])
+            nc.scalar.copy(
+                out=gx_t[k][:, h].bitcast(F32).rearrange("q (r p) u -> q r p u", r=R),
+                in_=xt[:].rearrange("q r u p -> q r p u"),
+            )
 
         def quant_x(k):
             gx = gx_t[k]
@@ -188,19 +190,17 @@ def tile_neuralobliviousdecisiontree_t_kernel(tc, x, W, b, leaf_values, out):
 
         def stage1_pe(k):
             cx, sx = cx_t[k]
-            zn = ps_z.tile([P, 2 * R, 2, TREES], F32, name="zn", tag="z")
-            for r in range(R):
-                for h in range(2):
-                    nc.tensor.matmul_mx(
-                        out=zn[:, 2 * r + h].rearrange("p j t -> p (j t)"),
-                        lhsT=cx[:, h, r * P : (r + 1) * P].bitcast(FP8X4),
-                        lhsT_scale=sx[:, h, r * P : (r + 1) * P],
-                        rhs=wcn[:].bitcast(FP8X4),
-                        rhs_scale=wsn[:],
-                        start=True,
-                        stop=True,
-                    )
-            zk = ps_z.tile([P, 2, NB], F32, name="zk", tag="z")
+            zr = ps_z.tile([P, 2 * NB], F32, name="zr", tag="zr")
+            nc.tensor.matmul_mx(
+                out=zr[:],
+                lhsT=wcn[:].bitcast(FP8X4),
+                lhsT_scale=wsn[:],
+                rhs=cx[:].rearrange("q h n -> q (h n)").bitcast(FP8X4),
+                rhs_scale=sx[:].rearrange("q h n -> q (h n)"),
+                start=True,
+                stop=True,
+            )
+            zk = ps_z.tile([P, 2, NB], F32, name="zk", tag="zk")
             for jj in range(2):
                 for v in range(2):
                     w0 = (v * 2 + jj) * P
@@ -213,63 +213,86 @@ def tile_neuralobliviousdecisiontree_t_kernel(tc, x, W, b, leaf_values, out):
                         start=(v == 0),
                         stop=(v == 1),
                     )
-            z_t[k] = (zn, zk)
+            z_t[k] = (zr, zk)
 
-        def bias_rows(k):
-            zn = z_t[k][0]
-            zb = q_pool.tile([P, 2, 2 * R, TREES], F32, name="zb")
-            nc.vector.tensor_tensor(
-                out=zb[:],
-                in0=zn[:].rearrange("p g j t -> p j g t"),
-                in1=bbc[:].unsqueeze(2).to_broadcast([P, 2, 2 * R, TREES]),
-                op=ALU.add,
+        def sigmoid_rows(k):
+            pr = q_pool.tile([P, 2 * NB], F32, name="pr")
+            nc.scalar.activation(
+                out=pr[:], in_=z_t[k][0][:], func=ACT.Sigmoid,
+                bias=bpos[:, DEPTH : DEPTH + 1], scale=1.0,
             )
-            qn = q_pool.tile([P, 2, 2, 2 * R * TREES], F32, name="qn")
-            for s in range(2):
-                nc.scalar.activation(
-                    out=qn[:, s].rearrange("p j c -> p (j c)"),
-                    in_=zb[:].rearrange("p j g t -> p (j g t)"),
-                    func=ACT.Sigmoid,
-                    scale=1.0 - 2.0 * s,
-                )
+            pr_t[k] = pr
+
+        def turn_rows(k):
+            zt = ps_z.tile([P, 2 * R, 2, TREES], F32, name="zt", tag="zt")
+            for r in range(R):
+                for h in range(2):
+                    c0 = h * NB + r * P
+                    nc.tensor.transpose(
+                        zt[:, 2 * r + h].rearrange("p j t -> p (j t)"),
+                        pr_t[k][:, c0 : c0 + P],
+                        ident[:],
+                    )
+            zt_t[k] = zt
+
+        def rows_out(k):
+            zt = zt_t[k]
+            qn = q_pool.tile([P, 2, 2, 2 * R, TREES], F32, name="qn")
+            nc.scalar.activation(out=qn[:, 0, 1], in_=zt[:, :, 1, :], func=ACT.Copy)
+            nc.scalar.activation(
+                out=qn[:, 1],
+                in_=zt[:].rearrange("p g j t -> p j g t"),
+                func=ACT.Copy,
+                scale=-1.0,
+                bias=1.0,
+            )
             qn_t[k] = qn
 
         def sigmoid_cols(k):
             zk = z_t[k][1]
             qk = q_pool.tile([P, 2, 2, NB], F32, name="qk")
-            for jj in range(2):
-                j = jj
+            for j in range(2):
                 nc.scalar.activation(
-                    out=qk[:, jj, 0, :], in_=zk[:, jj, :], func=ACT.Sigmoid,
+                    out=qk[:, j, 0, :], in_=zk[:, j, :], func=ACT.Sigmoid,
                     bias=bpos[:, j : j + 1], scale=1.0,
                 )
                 nc.scalar.activation(
-                    out=qk[:, jj, 1, :], in_=zk[:, jj, :], func=ACT.Sigmoid,
+                    out=qk[:, j, 1, :], in_=zk[:, j, :], func=ACT.Sigmoid,
                     bias=bneg[:, j : j + 1], scale=-1.0,
                 )
             qk_t[k] = qk
 
+        def factors_vector(k):
+            one = qn_t[k][:, 1, 0, 0, 0:1]
+            nc.vector.tensor_copy(out=one, in_=one)
+            an = an_pool.tile([P, 2, 2, 2 * R * TREES], F32, name="an")
+            bb = bb_pool.tile([P, 2, 2, NB], F32, name="bb")
+            f_t[k] = (an, bb)
+            nc.vector.tensor_tensor(
+                out=an[:, 0].rearrange("p c (g t) -> p c g t", t=TREES),
+                in0=zt_t[k][:, :, 0, :].unsqueeze(1).to_broadcast([P, 2, 2 * R, TREES]),
+                in1=qn_t[k][:, :, 1],
+                op=ALU.mult,
+            )
+
         def factors(k):
             qn = qn_t[k]
             qk = qk_t[k]
-            an = an_pool.tile([P, 2, 2, 2 * R * TREES], F32, name="an")
-            bb = bb_pool.tile([P, 2, 2, NB], F32, name="bb")
-            nc.gpsimd.tensor_tensor(
-                out=an[:],
-                in0=qn[:, :, 0, :].unsqueeze(2).to_broadcast([P, 2, 2, 2 * R * TREES]),
-                in1=qn[:, :, 1, :].unsqueeze(1).to_broadcast([P, 2, 2, 2 * R * TREES]),
+            an, bb = f_t[k]
+            eng = nc.vector if k == 0 else nc.gpsimd
+            eng.tensor_tensor(
+                out=an[:, 1],
+                in0=qn[:, 1, 0].rearrange("p g t -> p (g t)").unsqueeze(1)
+                .to_broadcast([P, 2, 2 * R * TREES]),
+                in1=qn[:, :, 1].rearrange("p s g t -> p s (g t)"),
                 op=ALU.mult,
             )
-            nc.gpsimd.tensor_tensor(
+            eng.tensor_tensor(
                 out=bb[:],
                 in0=qk[:, 0].unsqueeze(2).to_broadcast([P, 2, 2, NB]),
                 in1=qk[:, 1].unsqueeze(1).to_broadcast([P, 2, 2, NB]),
                 op=ALU.mult,
             )
-            f_t[k] = (an, bb)
-
-        def hold_gpsimd(k):
-            nc.gpsimd.memset(pa_t[k][:, 3, R - 1, P - 1, 2:4], 0.0)
 
         def flip(k, r):
             an = f_t[k][0]
@@ -336,46 +359,118 @@ def tile_neuralobliviousdecisiontree_t_kernel(tc, x, W, b, leaf_values, out):
                 in_=o[:],
             )
 
+        HW = CW // R
+        HG = GW // R
+        pe_t = {}
+
+        def product_last(r):
+            pe_t[r] = [
+                const.tile([P, 4, P, 4], BF16, name=f"pl{r}", align_bytes=64),
+                const.tile([P, 2 * HG], U32, name=f"ql{r}", align_bytes=64),
+                const.tile([P, HG], U32, name=f"al{r}", align_bytes=64),
+                const.tile([P, HG], U32, name=f"wl{r}", align_bytes=64),
+            ]
+            for g in range(2):
+                nc.gpsimd.memset(pe_t[r][1][:, g * HG + HW : (g + 1) * HG].bitcast(I32), 0)
+            nc.vector.tensor_tensor(
+                out=pe_t[r][0][:],
+                in0=a2_t[(last, r)][:].unsqueeze(1).to_broadcast([P, 4, P, 4]),
+                in1=f_t[last][1][:].rearrange("p s c n -> p (s c) n")[:, :, r * P : (r + 1) * P]
+                .unsqueeze(3).to_broadcast([P, 4, P, 4]),
+                op=ALU.mult,
+            )
+
+        def quant_last(r):
+            pl, ql, al, wl = pe_t[r]
+            for g in range(2):
+                nc.vector.quantize_mx(
+                    out=ql[:, g * HG : g * HG + HW].bitcast(FP8X4),
+                    scales=ql[:, g * HG + HW : (g + 1) * HG].bitcast(U8),
+                    in_=pl[:, 2 * g : 2 * g + 2].rearrange("p a n i -> p (a n i)"),
+                )
+            lo = slice(0, TREES)
+            hi = slice(TREES, 2 * TREES)
+            q = ql[:].bitcast(I32)
+            for dst, src in ((wl, hi), (al, lo)):
+                nc.sync.dma_start(out=dst[lo, :].bitcast(I32), in_=q[src, 0:HG])
+                nc.sync.dma_start(out=dst[hi, :].bitcast(I32), in_=q[src, HG : 2 * HG])
+
+        def stage2_last(r):
+            for h in (1, 0):
+                src = pe_t[r][3] if h == 1 else pe_t[r][2]
+                acc = ps_o.tile([P, DOUT], F32, name="acc")
+                for s in range(2):
+                    nc.tensor.matmul_mx(
+                        out=acc[:],
+                        lhsT=src[:, s * P : (s + 1) * P].bitcast(FP8X4),
+                        lhsT_scale=src[:, HW:HG].bitcast(U8)[:, s * P : (s + 1) * P],
+                        rhs=lc[:, s, :].bitcast(FP8X4),
+                        rhs_scale=ls[:, s, :],
+                        start=(s == 0),
+                        stop=(s == 1),
+                    )
+                ol = o_pool.tile([P, DOUT], F32, name="ol")
+                if h == 1:
+                    nc.vector.tensor_scalar(
+                        out=ol[:], in0=acc[:], scalar1=1.0 / TREES, scalar2=None, op0=ALU.mult
+                    )
+                else:
+                    nc.scalar.activation(out=ol[:], in_=acc[:], func=ACT.Copy, scale=1.0 / TREES)
+                row0 = h * HALF + last * NB
+                nc.sync.dma_start(
+                    out=out[row0 : row0 + NB, :].rearrange("(p r) d -> p r d", r=R)[:, r],
+                    in_=ol[:],
+                )
+
         def live(k):
             return 0 <= k < NBLK
 
-        last = NBLK - 1
         for i in range(-3, NBLK + 2):
             if 3 <= i + 6 < NBLK:
                 load_x(i + 6)
             if live(i + 1):
-                bias_rows(i + 1)
+                rows_out(i + 1)
             if live(i):
                 flip(i, 1)
             if live(i + 3):
-                transpose_x(i + 3)
-            if live(i - 2):
-                stage2(i - 2, 1)
+                transpose_x(i + 3, 0)
+            if i == -3:
+                bias_columns()
             if live(i + 2):
                 quant_x(i + 2)
                 stage1_pe(i + 2)
+                sigmoid_rows(i + 2)
+            if live(i - 3):
+                stage2(i - 3, 0)
+            if live(i + 2):
                 sigmoid_cols(i + 2)
-            if i == 1:
-                leaf_quant()
+            if live(i + 3):
+                transpose_x(i + 3, 1)
+            if live(i - 2) and i - 2 != last:
+                stage2(i - 2, 1)
+            if i == -2:
+                leaf_regroup(0)
+            if i == -1:
+                leaf_regroup(1)
             if live(i - 1) and i - 1 != last:
                 quant_path(i - 1, 0)
                 quant_path(i - 1, 1)
                 gather(i - 1)
-            if live(i - 2):
-                stage2(i - 2, 0)
-            if live(i - 1) and live(i + 1):
-                hold_gpsimd(i - 1)
             if live(i + 1):
+                factors_vector(i + 1)
                 factors(i + 1)
-            if i == 0:
-                for a in range(2):
-                    leaf_regroup(a)
+            if i == -1:
+                leaf_quant()
             if live(i):
-                product(i, 0)
-                product(i, 1)
-            if i == last:
-                quant_path(i, 0)
-                quant_path(i, 1)
-                gather(i)
+                for r in range(R):
+                    if i == last:
+                        product_last(r)
+                        quant_last(r)
+                    else:
+                        product(i, r)
             if live(i + 1):
                 flip(i + 1, 0)
+            if live(i + 2):
+                turn_rows(i + 2)
+        stage2_last(0)
+        stage2_last(1)

@@ -25,6 +25,8 @@ R = NB // P
 CW = 2 * R * P
 GW = CW + CW // 4
 RING = 5
+VC = 64
+GC = VC - 4
 NBLK = HALF // NB
 PIN = True
 
@@ -63,15 +65,16 @@ def tile_neuralobliviousdecisiontree_t_kernel(tc, x, W, b, leaf_values, out):
         f_t = {}
         a2_t = {}
         pa_t = {}
+        o_t = {}
 
         def load_x(k):
             xr = xr_pool.tile([P, 2, R * FEAT], BF16, name="xr")
-            if k == 0:
-                for h in range(2):
-                    nc.sync.dma_start(out=xr[:, h], in_=x_blk[k][:, h])
-            else:
-                nc.sync.dma_start(out=xr[:], in_=x_blk[k])
             xr_t[k] = xr
+            if k > 0:
+                nc.sync.dma_start(out=xr[:], in_=x_blk[k])
+
+        def load_first(h):
+            nc.sync.dma_start(out=xr_t[0][:, h], in_=x_blk[0][:, h])
 
         ident = const.tile([P, P], F32, name="ident")
         make_identity(nc, ident[:])
@@ -80,11 +83,12 @@ def tile_neuralobliviousdecisiontree_t_kernel(tc, x, W, b, leaf_values, out):
         bt = const.tile([P, P], BF16, name="bt")
         nc.gpsimd.memset(bt[:], 0.0)
         load_x(0)
+        load_first(0)
         nc.sync.dma_start(
             out=wr[:].rearrange("q j (u e) t -> q (j u) (e t)", u=2, e=2),
             in_=W.rearrange("j (u q e) t -> q (j u) (e t)", u=2, q=P, e=2),
         )
-        load_x(1)
+        load_first(1)
         for n in range(2):
             nc.sync.dma_start(out=bt[0:DEPTH, n * TREES : (n + 1) * TREES], in_=b)
         nc.sync.dma_start(
@@ -96,12 +100,18 @@ def tile_neuralobliviousdecisiontree_t_kernel(tc, x, W, b, leaf_values, out):
                 out=lr[u * TREES : (u + 1) * TREES],
                 in_=leaf_values[:, u * 8 : (u + 1) * 8, :],
             )
+        load_x(1)
         load_x(2)
 
         wg = const.tile([P, 2, 2, P, 4], BF16, name="wg", align_bytes=64)
         nc.gpsimd.memset(wg[:].rearrange("q v j m c -> q (v j m c)").bitcast(I32), 0)
         lc = const.tile([P, 2, DOUT], U32, name="lc", align_bytes=64)
         ls = const.tile([P, 2, DOUT], U8, name="ls", align_bytes=64)
+        lz = const.tile([P, 2, 4, DOUT], U32, name="lz", align_bytes=64)
+        lzs = const.tile([P, 2, 4, DOUT], U8, name="lzs", align_bytes=64)
+        zero = const.tile([P, DOUT], U32, name="zero")
+        nc.gpsimd.memset(zero[:].bitcast(I32), 0)
+        nc.gpsimd.memset(ls[:].rearrange("p s d -> p (s d)").bitcast(I32), 0)
         pt_ring = []
         wt_ring = []
         for n in range(RING):
@@ -236,16 +246,10 @@ def tile_neuralobliviousdecisiontree_t_kernel(tc, x, W, b, leaf_values, out):
             zt_t[k] = zt
 
         def rows_out(k):
-            zt = zt_t[k]
+            zt = zt_t[k][:].rearrange("p g j t -> p j g t")
             qn = q_pool.tile([P, 2, 2, 2 * R, TREES], F32, name="qn")
-            nc.scalar.activation(out=qn[:, 0, 1], in_=zt[:, :, 1, :], func=ACT.Copy)
-            nc.scalar.activation(
-                out=qn[:, 1],
-                in_=zt[:].rearrange("p g j t -> p j g t"),
-                func=ACT.Copy,
-                scale=-1.0,
-                bias=1.0,
-            )
+            nc.scalar.activation(out=qn[:, 0], in_=zt, func=ACT.Copy)
+            nc.scalar.activation(out=qn[:, 1], in_=zt, func=ACT.Copy, scale=-1.0, bias=1.0)
             qn_t[k] = qn
 
         def sigmoid_cols(k):
@@ -262,31 +266,27 @@ def tile_neuralobliviousdecisiontree_t_kernel(tc, x, W, b, leaf_values, out):
                 )
             qk_t[k] = qk
 
-        def factors_vector(k):
-            one = qn_t[k][:, 1, 0, 0, 0:1]
-            nc.vector.tensor_copy(out=one, in_=one)
-            an = an_pool.tile([P, 2, 2, 2 * R * TREES], F32, name="an")
-            bb = bb_pool.tile([P, 2, 2, NB], F32, name="bb")
-            f_t[k] = (an, bb)
-            nc.vector.tensor_tensor(
-                out=an[:, 0].rearrange("p c (g t) -> p c g t", t=TREES),
-                in0=zt_t[k][:, :, 0, :].unsqueeze(1).to_broadcast([P, 2, 2 * R, TREES]),
-                in1=qn_t[k][:, :, 1],
+        def row_product(eng, k, c0, c1):
+            qn = qn_t[k][:].rearrange("p s j g t -> p s j (g t)")
+            shape = [P, 2, 2, c1 - c0]
+            eng.tensor_tensor(
+                out=f_t[k][0][:, :, :, c0:c1],
+                in0=qn[:, :, 0, c0:c1].unsqueeze(2).to_broadcast(shape),
+                in1=qn[:, :, 1, c0:c1].unsqueeze(1).to_broadcast(shape),
                 op=ALU.mult,
             )
 
         def factors(k):
-            qn = qn_t[k]
+            an = an_pool.tile([P, 2, 2, 2 * R * TREES], F32, name="an")
+            bb = bb_pool.tile([P, 2, 2, NB], F32, name="bb")
+            f_t[k] = (an, bb)
             qk = qk_t[k]
-            an, bb = f_t[k]
+            if k == 0:
+                row_product(nc.vector, k, 0, NB)
+            else:
+                row_product(nc.vector, k, 0, VC)
+                row_product(nc.gpsimd, k, GC, NB)
             eng = nc.vector if k == 0 else nc.gpsimd
-            eng.tensor_tensor(
-                out=an[:, 1],
-                in0=qn[:, 1, 0].rearrange("p g t -> p (g t)").unsqueeze(1)
-                .to_broadcast([P, 2, 2 * R * TREES]),
-                in1=qn[:, :, 1].rearrange("p s g t -> p s (g t)"),
-                op=ALU.mult,
-            )
             eng.tensor_tensor(
                 out=bb[:],
                 in0=qk[:, 0].unsqueeze(2).to_broadcast([P, 2, 2, NB]),
@@ -332,7 +332,12 @@ def tile_neuralobliviousdecisiontree_t_kernel(tc, x, W, b, leaf_values, out):
             hi = slice(TREES, 2 * TREES)
             nc.sync.dma_start(out=wt[lo, :], in_=pt[hi, 0:GW])
             nc.sync.dma_start(out=wt[hi, :], in_=pt[hi, GW : 2 * GW])
-            nc.sync.dma_start(out=pt[hi, 0:GW], in_=pt[lo, GW : 2 * GW])
+
+        def gather_rest(k):
+            pt = pt_ring[k % RING][:].bitcast(I32)
+            nc.sync.dma_start(
+                out=pt[TREES : 2 * TREES, 0:GW], in_=pt[0:TREES, GW : 2 * GW]
+            )
 
         def stage2(k, h):
             src = wt_ring[k % RING] if h == 1 else pt_ring[k % RING]
@@ -350,64 +355,80 @@ def tile_neuralobliviousdecisiontree_t_kernel(tc, x, W, b, leaf_values, out):
                         start=(s == 0),
                         stop=(s == 1),
                     )
-                nc.scalar.activation(
-                    out=o[:, r, :], in_=acc[:], func=ACT.Copy, scale=1.0 / TREES
-                )
+                if k == last - 1 and h == 0:
+                    nc.vector.tensor_scalar(
+                        out=o[:, r, :], in0=acc[:], scalar1=1.0 / TREES, scalar2=None, op0=ALU.mult
+                    )
+                else:
+                    nc.scalar.activation(
+                        out=o[:, r, :], in_=acc[:], func=ACT.Copy, scale=1.0 / TREES
+                    )
+            o_t[(k, h)] = o
+
+        def store(k, h):
             row0 = h * HALF + k * NB
             nc.sync.dma_start(
                 out=out[row0 : row0 + NB, :].rearrange("(p r) d -> p r d", r=R),
-                in_=o[:],
+                in_=o_t[(k, h)][:],
             )
 
-        HW = CW // R
-        HG = GW // R
-        pe_t = {}
+        def leaf_stuffed(step):
+            h, n = divmod(step, 4)
+            halves = (slice(0, TREES), slice(TREES, 2 * TREES))
+            this, other = halves[h], halves[1 - h]
+            scales = lzs[:].rearrange("p h a d -> p h (a d)").bitcast(I32)
+            one = ls[:].rearrange("p s d -> p (s d)").bitcast(I32)
+            if n < 2:
+                src = zero[other, :].bitcast(I32).unsqueeze(1).to_broadcast([TREES, 2, DOUT])
+                nc.sync.dma_start(out=lz[other, h, 2 * n : 2 * n + 2, :].bitcast(I32), in_=src)
+                if n == 0:
+                    nc.sync.dma_start(out=scales[other, h], in_=zero[other, :].bitcast(I32))
+            else:
+                u = n - 2
+                nc.sync.dma_start(
+                    out=lz[this, h, 2 * u : 2 * u + 2, :].bitcast(I32),
+                    in_=lc[halves[u], :, :].bitcast(I32),
+                )
+                nc.sync.dma_start(
+                    out=scales[this, h, u * (DOUT // 2) : (u + 1) * (DOUT // 2)],
+                    in_=one[halves[u], :],
+                )
+
+        pl_t = {}
 
         def product_last(r):
-            pe_t[r] = [
-                const.tile([P, 4, P, 4], BF16, name=f"pl{r}", align_bytes=64),
-                const.tile([P, 2 * HG], U32, name=f"ql{r}", align_bytes=64),
-                const.tile([P, HG], U32, name=f"al{r}", align_bytes=64),
-                const.tile([P, HG], U32, name=f"wl{r}", align_bytes=64),
-            ]
-            for g in range(2):
-                nc.gpsimd.memset(pe_t[r][1][:, g * HG + HW : (g + 1) * HG].bitcast(I32), 0)
+            pl = const.tile([P, 4, P, 4], BF16, name=f"pl{r}", align_bytes=64)
+            ql = const.tile([P, 4, P], U32, name=f"ql{r}", align_bytes=64)
+            sl = const.tile([P, 4, P], U8, name=f"sl{r}", align_bytes=64)
+            pl_t[r] = (ql, sl)
             nc.vector.tensor_tensor(
-                out=pe_t[r][0][:],
+                out=pl[:],
                 in0=a2_t[(last, r)][:].unsqueeze(1).to_broadcast([P, 4, P, 4]),
                 in1=f_t[last][1][:].rearrange("p s c n -> p (s c) n")[:, :, r * P : (r + 1) * P]
                 .unsqueeze(3).to_broadcast([P, 4, P, 4]),
                 op=ALU.mult,
             )
-
-        def quant_last(r):
-            pl, ql, al, wl = pe_t[r]
-            for g in range(2):
-                nc.vector.quantize_mx(
-                    out=ql[:, g * HG : g * HG + HW].bitcast(FP8X4),
-                    scales=ql[:, g * HG + HW : (g + 1) * HG].bitcast(U8),
-                    in_=pl[:, 2 * g : 2 * g + 2].rearrange("p a n i -> p (a n i)"),
-                )
-            lo = slice(0, TREES)
-            hi = slice(TREES, 2 * TREES)
-            q = ql[:].bitcast(I32)
-            for dst, src in ((wl, hi), (al, lo)):
-                nc.sync.dma_start(out=dst[lo, :].bitcast(I32), in_=q[src, 0:HG])
-                nc.sync.dma_start(out=dst[hi, :].bitcast(I32), in_=q[src, HG : 2 * HG])
+            nc.vector.quantize_mx(
+                out=ql[:].rearrange("p a n -> p (a n)").bitcast(FP8X4),
+                scales=sl[:].rearrange("p a n -> p (a n)"),
+                in_=pl[:].rearrange("p a n i -> p (a n i)"),
+            )
 
         def stage2_last(r):
-            for h in (1, 0):
-                src = pe_t[r][3] if h == 1 else pe_t[r][2]
-                acc = ps_o.tile([P, DOUT], F32, name="acc")
-                for s in range(2):
+            ql, sl = pl_t[r]
+            for h in range(2):
+                tag = (("zr", "zk"), ("zt", "xt"))[r][h]
+                bank = ps_x if tag == "xt" else ps_z
+                acc = bank.tile([P, DOUT], F32, name="acc_last", tag=tag)
+                for a in range(4):
                     nc.tensor.matmul_mx(
                         out=acc[:],
-                        lhsT=src[:, s * P : (s + 1) * P].bitcast(FP8X4),
-                        lhsT_scale=src[:, HW:HG].bitcast(U8)[:, s * P : (s + 1) * P],
-                        rhs=lc[:, s, :].bitcast(FP8X4),
-                        rhs_scale=ls[:, s, :],
-                        start=(s == 0),
-                        stop=(s == 1),
+                        lhsT=ql[:, a, :].bitcast(FP8X4),
+                        lhsT_scale=sl[:, a, :],
+                        rhs=lz[:, h, a, :].bitcast(FP8X4),
+                        rhs_scale=lzs[:, h, a, :],
+                        start=(a == 0),
+                        stop=(a == 3),
                     )
                 ol = o_pool.tile([P, DOUT], F32, name="ol")
                 if h == 1:
@@ -428,6 +449,8 @@ def tile_neuralobliviousdecisiontree_t_kernel(tc, x, W, b, leaf_values, out):
         for i in range(-3, NBLK + 2):
             if 3 <= i + 6 < NBLK:
                 load_x(i + 6)
+            if live(i - 2) and i - 2 != last:
+                gather_rest(i - 2)
             if live(i + 1):
                 rows_out(i + 1)
             if live(i):
@@ -450,27 +473,31 @@ def tile_neuralobliviousdecisiontree_t_kernel(tc, x, W, b, leaf_values, out):
                 stage2(i - 2, 1)
             if i == -2:
                 leaf_regroup(0)
-            if i == -1:
-                leaf_regroup(1)
             if live(i - 1) and i - 1 != last:
                 quant_path(i - 1, 0)
                 quant_path(i - 1, 1)
                 gather(i - 1)
             if live(i + 1):
-                factors_vector(i + 1)
                 factors(i + 1)
+            if 4 <= i < 12:
+                leaf_stuffed(i - 4)
             if i == -1:
+                leaf_regroup(1)
                 leaf_quant()
             if live(i):
                 for r in range(R):
                     if i == last:
                         product_last(r)
-                        quant_last(r)
                     else:
                         product(i, r)
             if live(i + 1):
                 flip(i + 1, 0)
             if live(i + 2):
                 turn_rows(i + 2)
-        stage2_last(0)
+            if live(i - 3):
+                store(i - 3, 0)
+            if live(i - 2) and i - 2 != last:
+                store(i - 2, 1)
+            if i == NBLK:
+                stage2_last(0)
         stage2_last(1)

@@ -23,10 +23,8 @@ HALF = ROWS // 2
 NB = 256
 R = NB // P
 CW = 2 * R * P
-GW = CW + CW // 4
+SW = CW // 4
 RING = 5
-VC = 64
-GC = VC - 4
 NBLK = HALF // NB
 PIN = True
 
@@ -43,9 +41,7 @@ def tile_neuralobliviousdecisiontree_t_kernel(tc, x, W, b, leaf_values, out):
         gx_pool = ctx.enter_context(tc.tile_pool(name="gx", bufs=2))
         cx_pool = ctx.enter_context(tc.tile_pool(name="cx", bufs=2))
         q_pool = ctx.enter_context(tc.tile_pool(name="q", bufs=2))
-        an_pool = ctx.enter_context(tc.tile_pool(name="an", bufs=2))
         bb_pool = ctx.enter_context(tc.tile_pool(name="bb", bufs=2))
-        pa_pool = ctx.enter_context(tc.tile_pool(name="pa", bufs=2))
         o_pool = ctx.enter_context(tc.tile_pool(name="o", bufs=4))
         ps_x = ctx.enter_context(tc.psum_pool(name="psx", bufs=1))
         ps_z = ctx.enter_context(tc.psum_pool(name="psz", bufs=1))
@@ -62,9 +58,8 @@ def tile_neuralobliviousdecisiontree_t_kernel(tc, x, W, b, leaf_values, out):
         zt_t = {}
         qn_t = {}
         qk_t = {}
-        f_t = {}
+        bb_t = {}
         a2_t = {}
-        pa_t = {}
         o_t = {}
 
         def load_x(k):
@@ -115,12 +110,23 @@ def tile_neuralobliviousdecisiontree_t_kernel(tc, x, W, b, leaf_values, out):
         pt_ring = []
         wt_ring = []
         for n in range(RING):
-            pt = const.tile([P, 2 * GW], U32, name=f"pt{n}", align_bytes=64)
-            wt = const.tile([P, GW], U32, name=f"wt{n}", align_bytes=64)
-            for g in range(2):
-                nc.gpsimd.memset(pt[:, g * GW + CW : (g + 1) * GW].bitcast(I32), 0)
+            pt = const.tile([P, 2 * CW + 2 * SW], U32, name=f"pt{n}", align_bytes=64)
+            wt = const.tile([P, CW + SW], U32, name=f"wt{n}", align_bytes=64)
+            nc.gpsimd.memset(pt[:, 2 * CW :].bitcast(I32), 0)
             pt_ring.append(pt)
             wt_ring.append(wt)
+
+        mix = [
+            const.tile([P, 2 * R * P * 4], F32, name=f"mix{n}", align_bytes=64) for n in range(3)
+        ]
+
+        def path(k):
+            return mix[k % 3][:].bitcast(BF16).rearrange(
+                "p (a r n i) -> p a r n i", a=4, r=R, i=4
+            )
+
+        def rows_factor(k):
+            return mix[(k + 1) % 3][:, 0 : 4 * NB].rearrange("p (s c n) -> p s c n", s=2, c=2)
 
         wgn = const.tile([P, 2, TREES, 4], BF16, name="wgn", align_bytes=64)
         nc.vector.tensor_copy(out=wgn[:], in_=wr[:, 2:4].rearrange("q j c t -> q j t c"))
@@ -266,81 +272,73 @@ def tile_neuralobliviousdecisiontree_t_kernel(tc, x, W, b, leaf_values, out):
                 )
             qk_t[k] = qk
 
-        def row_product(eng, k, c0, c1):
+        def factors(k):
+            eng = nc.vector if k == 0 else nc.gpsimd
             qn = qn_t[k][:].rearrange("p s j g t -> p s j (g t)")
-            shape = [P, 2, 2, c1 - c0]
             eng.tensor_tensor(
-                out=f_t[k][0][:, :, :, c0:c1],
-                in0=qn[:, :, 0, c0:c1].unsqueeze(2).to_broadcast(shape),
-                in1=qn[:, :, 1, c0:c1].unsqueeze(1).to_broadcast(shape),
+                out=rows_factor(k),
+                in0=qn[:, :, 0].unsqueeze(2).to_broadcast([P, 2, 2, NB]),
+                in1=qn[:, :, 1].unsqueeze(1).to_broadcast([P, 2, 2, NB]),
                 op=ALU.mult,
             )
-
-        def factors(k):
-            an = an_pool.tile([P, 2, 2, 2 * R * TREES], F32, name="an")
             bb = bb_pool.tile([P, 2, 2, NB], F32, name="bb")
-            f_t[k] = (an, bb)
             qk = qk_t[k]
-            if k == 0:
-                row_product(nc.vector, k, 0, NB)
-            else:
-                row_product(nc.vector, k, 0, VC)
-                row_product(nc.gpsimd, k, GC, NB)
-            eng = nc.vector if k == 0 else nc.gpsimd
             eng.tensor_tensor(
                 out=bb[:],
                 in0=qk[:, 0].unsqueeze(2).to_broadcast([P, 2, 2, NB]),
                 in1=qk[:, 1].unsqueeze(1).to_broadcast([P, 2, 2, NB]),
                 op=ALU.mult,
             )
+            bb_t[k] = bb
 
         def flip(k, r):
-            an = f_t[k][0]
             a2 = ps_a.tile([P, P, 4], F32, name="a2")
             for a in range(4):
                 nc.tensor.transpose(
                     a2[:, :, a],
-                    an[:].rearrange("p s c n -> p (s c) n")[:, a, r * P : (r + 1) * P],
+                    rows_factor(k)[:, a // 2, a % 2, r * P : (r + 1) * P],
                     ident[:],
                 )
             a2_t[(k, r)] = a2
 
-        def product(k, r):
-            bb = f_t[k][1]
-            if r == 0:
-                pa_t[k] = pa_pool.tile([P, 4, R, P, 4], BF16, name="pa", align_bytes=64)
+        def product(k, r, dst):
             nc.vector.tensor_tensor(
-                out=pa_t[k][:, :, r],
+                out=dst,
                 in0=a2_t[(k, r)][:].unsqueeze(1).to_broadcast([P, 4, P, 4]),
-                in1=bb[:].rearrange("p s c n -> p (s c) n")[:, :, r * P : (r + 1) * P]
+                in1=bb_t[k][:].rearrange("p s c n -> p (s c) n")[:, :, r * P : (r + 1) * P]
                 .unsqueeze(3).to_broadcast([P, 4, P, 4]),
                 op=ALU.mult,
             )
 
-        def quant_path(k, g):
+        def quant_path(k):
             pt = pt_ring[k % RING]
             nc.vector.quantize_mx(
-                out=pt[:, g * GW : g * GW + CW].bitcast(FP8X4),
-                scales=pt[:, g * GW + CW : (g + 1) * GW].bitcast(U8),
-                in_=pa_t[k][:, 2 * g : 2 * g + 2].rearrange("p a r n i -> p (a r n i)"),
+                out=pt[:, 0 : 2 * CW].bitcast(FP8X4),
+                scales=pt[:, 2 * CW :].bitcast(U8),
+                in_=mix[k % 3][:].bitcast(BF16),
             )
+
+        lo = slice(0, TREES)
+        hi = slice(TREES, 2 * TREES)
+        first = (slice(0, CW), slice(2 * CW, 2 * CW + SW))
+        second = (slice(CW, 2 * CW), slice(2 * CW + SW, 2 * CW + 2 * SW))
+        packed = (slice(0, CW), slice(CW, CW + SW))
 
         def gather(k):
             pt = pt_ring[k % RING][:].bitcast(I32)
             wt = wt_ring[k % RING][:].bitcast(I32)
-            lo = slice(0, TREES)
-            hi = slice(TREES, 2 * TREES)
-            nc.sync.dma_start(out=wt[lo, :], in_=pt[hi, 0:GW])
-            nc.sync.dma_start(out=wt[hi, :], in_=pt[hi, GW : 2 * GW])
+            for n in range(2):
+                nc.sync.dma_start(out=wt[lo, packed[n]], in_=pt[hi, first[n]])
+                nc.sync.dma_start(out=wt[hi, packed[n]], in_=pt[hi, second[n]])
 
         def gather_rest(k):
             pt = pt_ring[k % RING][:].bitcast(I32)
-            nc.sync.dma_start(
-                out=pt[TREES : 2 * TREES, 0:GW], in_=pt[0:TREES, GW : 2 * GW]
-            )
+            for n in range(2):
+                nc.sync.dma_start(out=pt[hi, first[n]], in_=pt[lo, second[n]])
 
         def stage2(k, h):
             src = wt_ring[k % RING] if h == 1 else pt_ring[k % RING]
+            scales = src[:, (packed if h == 1 else first)[1]].bitcast(U8)
             o = o_pool.tile([P, R, DOUT], F32, name="o")
             for r in range(R):
                 acc = ps_o.tile([P, DOUT], F32, name="acc")
@@ -349,7 +347,7 @@ def tile_neuralobliviousdecisiontree_t_kernel(tc, x, W, b, leaf_values, out):
                     nc.tensor.matmul_mx(
                         out=acc[:],
                         lhsT=src[:, c0 : c0 + P].bitcast(FP8X4),
-                        lhsT_scale=src[:, CW : GW].bitcast(U8)[:, c0 : c0 + P],
+                        lhsT_scale=scales[:, c0 : c0 + P],
                         rhs=lc[:, s, :].bitcast(FP8X4),
                         rhs_scale=ls[:, s, :],
                         start=(s == 0),
@@ -401,13 +399,7 @@ def tile_neuralobliviousdecisiontree_t_kernel(tc, x, W, b, leaf_values, out):
             ql = const.tile([P, 4, P], U32, name=f"ql{r}", align_bytes=64)
             sl = const.tile([P, 4, P], U8, name=f"sl{r}", align_bytes=64)
             pl_t[r] = (ql, sl)
-            nc.vector.tensor_tensor(
-                out=pl[:],
-                in0=a2_t[(last, r)][:].unsqueeze(1).to_broadcast([P, 4, P, 4]),
-                in1=f_t[last][1][:].rearrange("p s c n -> p (s c) n")[:, :, r * P : (r + 1) * P]
-                .unsqueeze(3).to_broadcast([P, 4, P, 4]),
-                op=ALU.mult,
-            )
+            product(last, r, pl[:])
             nc.vector.quantize_mx(
                 out=ql[:].rearrange("p a n -> p (a n)").bitcast(FP8X4),
                 scales=sl[:].rearrange("p a n -> p (a n)"),
@@ -474,8 +466,7 @@ def tile_neuralobliviousdecisiontree_t_kernel(tc, x, W, b, leaf_values, out):
             if i == -2:
                 leaf_regroup(0)
             if live(i - 1) and i - 1 != last:
-                quant_path(i - 1, 0)
-                quant_path(i - 1, 1)
+                quant_path(i - 1)
                 gather(i - 1)
             if live(i + 1):
                 factors(i + 1)
@@ -489,7 +480,7 @@ def tile_neuralobliviousdecisiontree_t_kernel(tc, x, W, b, leaf_values, out):
                     if i == last:
                         product_last(r)
                     else:
-                        product(i, r)
+                        product(i, r, path(i)[:, :, r])
             if live(i + 1):
                 flip(i + 1, 0)
             if live(i + 2):

@@ -38,7 +38,7 @@ def tile_neuralobliviousdecisiontree_t_kernel(tc, x, W, b, leaf_values, out):
             ctx.enter_context(tc.manual_schedule())
         const = ctx.enter_context(tc.tile_pool(name="const", bufs=1))
         xr_pool = ctx.enter_context(tc.tile_pool(name="xr", bufs=4))
-        gx_pool = ctx.enter_context(tc.tile_pool(name="gx", bufs=2))
+        pa_pool = ctx.enter_context(tc.tile_pool(name="pa", bufs=2))
         cx_pool = ctx.enter_context(tc.tile_pool(name="cx", bufs=2))
         q_pool = ctx.enter_context(tc.tile_pool(name="q", bufs=2))
         bb_pool = ctx.enter_context(tc.tile_pool(name="bb", bufs=2))
@@ -51,7 +51,7 @@ def tile_neuralobliviousdecisiontree_t_kernel(tc, x, W, b, leaf_values, out):
         x_blk = x.rearrange("(h k p r) f -> k p h (r f)", h=2, k=NBLK, p=P, r=R)
 
         xr_t = {}
-        gx_t = {}
+        pa_t = {}
         cx_t = {}
         z_t = {}
         pr_t = {}
@@ -116,17 +116,13 @@ def tile_neuralobliviousdecisiontree_t_kernel(tc, x, W, b, leaf_values, out):
             pt_ring.append(pt)
             wt_ring.append(wt)
 
-        mix = [
-            const.tile([P, 2 * R * P * 4], F32, name=f"mix{n}", align_bytes=64) for n in range(3)
-        ]
+        ring = [const.tile([P, 4 * NB], F32, name=f"ring{n}", align_bytes=64) for n in range(3)]
 
-        def path(k):
-            return mix[k % 3][:].bitcast(BF16).rearrange(
-                "p (a r n i) -> p a r n i", a=4, r=R, i=4
-            )
+        def grouped(k):
+            return ring[k % 3][:].rearrange("q (h n u) -> q h n u", h=2, u=2)
 
         def rows_factor(k):
-            return mix[(k + 1) % 3][:, 0 : 4 * NB].rearrange("p (s c n) -> p s c n", s=2, c=2)
+            return ring[(k + 1) % 3][:].rearrange("p (s c n) -> p s c n", s=2, c=2)
 
         wgn = const.tile([P, 2, TREES, 4], BF16, name="wgn", align_bytes=64)
         nc.vector.tensor_copy(out=wgn[:], in_=wr[:, 2:4].rearrange("q j c t -> q j t c"))
@@ -180,8 +176,6 @@ def tile_neuralobliviousdecisiontree_t_kernel(tc, x, W, b, leaf_values, out):
         last = NBLK - 1
 
         def transpose_x(k, h):
-            if h == 0:
-                gx_t[k] = gx_pool.tile([P, 2, NB, 4], BF16, name="gx", align_bytes=64)
             xt = ps_x.tile([P, R, 2, P], F32, name="xt", tag="xt")
             xw = xr_t[k][:, h, :].bitcast(F32)
             for r in range(R):
@@ -189,18 +183,17 @@ def tile_neuralobliviousdecisiontree_t_kernel(tc, x, W, b, leaf_values, out):
                     c0 = r * (FEAT // 2) + u * P
                     nc.tensor.transpose(xt[:, r, u, :], xw[:, c0 : c0 + P], ident[:])
             nc.scalar.copy(
-                out=gx_t[k][:, h].bitcast(F32).rearrange("q (r p) u -> q r p u", r=R),
+                out=grouped(k)[:, h].rearrange("q (r p) u -> q r p u", r=R),
                 in_=xt[:].rearrange("q r u p -> q r p u"),
             )
 
         def quant_x(k):
-            gx = gx_t[k]
             cx = cx_pool.tile([P, 2, NB], U32, name="cx", align_bytes=64)
             sx = cx_pool.tile([P, 2, NB], U8, name="sx", align_bytes=64)
             nc.vector.quantize_mx(
                 out=cx[:].rearrange("q h n -> q (h n)").bitcast(FP8X4),
                 scales=sx[:].rearrange("q h n -> q (h n)"),
-                in_=gx[:].rearrange("q h n c -> q (h n c)"),
+                in_=ring[k % 3][:].bitcast(BF16),
             )
             cx_t[k] = (cx, sx)
 
@@ -301,12 +294,13 @@ def tile_neuralobliviousdecisiontree_t_kernel(tc, x, W, b, leaf_values, out):
                 )
             a2_t[(k, r)] = a2
 
-        def product(k, r, dst):
+        def product(k, r, dst, groups=slice(0, 4)):
+            shape = [P, groups.stop - groups.start, P, 4]
             nc.vector.tensor_tensor(
                 out=dst,
-                in0=a2_t[(k, r)][:].unsqueeze(1).to_broadcast([P, 4, P, 4]),
-                in1=bb_t[k][:].rearrange("p s c n -> p (s c) n")[:, :, r * P : (r + 1) * P]
-                .unsqueeze(3).to_broadcast([P, 4, P, 4]),
+                in0=a2_t[(k, r)][:].unsqueeze(1).to_broadcast(shape),
+                in1=bb_t[k][:].rearrange("p s c n -> p (s c) n")[:, groups, r * P : (r + 1) * P]
+                .unsqueeze(3).to_broadcast(shape),
                 op=ALU.mult,
             )
 
@@ -315,7 +309,7 @@ def tile_neuralobliviousdecisiontree_t_kernel(tc, x, W, b, leaf_values, out):
             nc.vector.quantize_mx(
                 out=pt[:, 0 : 2 * CW].bitcast(FP8X4),
                 scales=pt[:, 2 * CW :].bitcast(U8),
-                in_=mix[k % 3][:].bitcast(BF16),
+                in_=pa_t[k][:].rearrange("p a r n i -> p (a r n i)"),
             )
 
         lo = slice(0, TREES)
@@ -331,14 +325,27 @@ def tile_neuralobliviousdecisiontree_t_kernel(tc, x, W, b, leaf_values, out):
                 nc.sync.dma_start(out=wt[lo, packed[n]], in_=pt[hi, first[n]])
                 nc.sync.dma_start(out=wt[hi, packed[n]], in_=pt[hi, second[n]])
 
+        own_t = {}
+
         def gather_rest(k):
             pt = pt_ring[k % RING][:].bitcast(I32)
+            if k < last - 1:
+                for n in range(2):
+                    nc.sync.dma_start(out=pt[hi, first[n]], in_=pt[lo, second[n]])
+                return
+            own_t[k] = wt_ring[(k + 1) % RING]
+            at = own_t[k][:].bitcast(I32)
             for n in range(2):
-                nc.sync.dma_start(out=pt[hi, first[n]], in_=pt[lo, second[n]])
+                nc.sync.dma_start(out=at[lo, packed[n]], in_=pt[lo, first[n]])
+                nc.sync.dma_start(out=at[hi, packed[n]], in_=pt[lo, second[n]])
 
         def stage2(k, h):
-            src = wt_ring[k % RING] if h == 1 else pt_ring[k % RING]
-            scales = src[:, (packed if h == 1 else first)[1]].bitcast(U8)
+            if h == 1 or k in own_t:
+                src = wt_ring[k % RING] if h == 1 else own_t[k]
+                scales = src[:, packed[1]].bitcast(U8)
+            else:
+                src = pt_ring[k % RING]
+                scales = src[:, first[1]].bitcast(U8)
             o = o_pool.tile([P, R, DOUT], F32, name="o")
             for r in range(R):
                 acc = ps_o.tile([P, DOUT], F32, name="acc")
@@ -399,29 +406,37 @@ def tile_neuralobliviousdecisiontree_t_kernel(tc, x, W, b, leaf_values, out):
             ql = const.tile([P, 4, P], U32, name=f"ql{r}", align_bytes=64)
             sl = const.tile([P, 4, P], U8, name=f"sl{r}", align_bytes=64)
             pl_t[r] = (ql, sl)
-            product(last, r, pl[:])
-            nc.vector.quantize_mx(
-                out=ql[:].rearrange("p a n -> p (a n)").bitcast(FP8X4),
-                scales=sl[:].rearrange("p a n -> p (a n)"),
-                in_=pl[:].rearrange("p a n i -> p (a n i)"),
-            )
+            parts = [slice(0, 4)] if r == 0 else [slice(0, 2), slice(2, 4)]
+            for part in parts:
+                product(last, r, pl[:, part], part)
+            for part in parts:
+                nc.vector.quantize_mx(
+                    out=ql[:, part].rearrange("p a n -> p (a n)").bitcast(FP8X4),
+                    scales=sl[:, part].rearrange("p a n -> p (a n)"),
+                    in_=pl[:, part].rearrange("p a n i -> p (a n i)"),
+                )
 
         def stage2_last(r):
             ql, sl = pl_t[r]
+            accs = []
             for h in range(2):
                 tag = (("zr", "zk"), ("zt", "xt"))[r][h]
                 bank = ps_x if tag == "xt" else ps_z
-                acc = bank.tile([P, DOUT], F32, name="acc_last", tag=tag)
-                for a in range(4):
-                    nc.tensor.matmul_mx(
-                        out=acc[:],
-                        lhsT=ql[:, a, :].bitcast(FP8X4),
-                        lhsT_scale=sl[:, a, :],
-                        rhs=lz[:, h, a, :].bitcast(FP8X4),
-                        rhs_scale=lzs[:, h, a, :],
-                        start=(a == 0),
-                        stop=(a == 3),
-                    )
+                accs.append(bank.tile([P, DOUT], F32, name="acc_last", tag=tag))
+            for part in ([range(0, 4)] if r == 0 else [range(0, 2), range(2, 4)]):
+                for h in range(2):
+                    for a in part:
+                        nc.tensor.matmul_mx(
+                            out=accs[h][:],
+                            lhsT=ql[:, a, :].bitcast(FP8X4),
+                            lhsT_scale=sl[:, a, :],
+                            rhs=lz[:, h, a, :].bitcast(FP8X4),
+                            rhs_scale=lzs[:, h, a, :],
+                            start=(a == 0),
+                            stop=(a == 3),
+                        )
+            for h in range(2):
+                acc = accs[h]
                 ol = o_pool.tile([P, DOUT], F32, name="ol")
                 if h == 1:
                     nc.vector.tensor_scalar(
@@ -438,10 +453,10 @@ def tile_neuralobliviousdecisiontree_t_kernel(tc, x, W, b, leaf_values, out):
         def live(k):
             return 0 <= k < NBLK
 
-        for i in range(-3, NBLK + 2):
+        for i in range(-3, NBLK + 1):
             if 3 <= i + 6 < NBLK:
                 load_x(i + 6)
-            if live(i - 2) and i - 2 != last:
+            if live(i - 2) and i - 2 < last - 1:
                 gather_rest(i - 2)
             if live(i + 1):
                 rows_out(i + 1)
@@ -455,40 +470,48 @@ def tile_neuralobliviousdecisiontree_t_kernel(tc, x, W, b, leaf_values, out):
                 quant_x(i + 2)
                 stage1_pe(i + 2)
                 sigmoid_rows(i + 2)
-            if live(i - 3):
+            if live(i - 3) and i - 3 < last - 1:
                 stage2(i - 3, 0)
             if live(i + 2):
                 sigmoid_cols(i + 2)
             if live(i + 3):
                 transpose_x(i + 3, 1)
+            if i == NBLK:
+                stage2_last(0)
             if live(i - 2) and i - 2 != last:
                 stage2(i - 2, 1)
+                if i - 2 == last - 1:
+                    stage2(i - 2, 0)
             if i == -2:
                 leaf_regroup(0)
+                leaf_regroup(1)
             if live(i - 1) and i - 1 != last:
                 quant_path(i - 1)
                 gather(i - 1)
+                if i - 1 == last - 1:
+                    gather_rest(i - 1)
             if live(i + 1):
                 factors(i + 1)
             if 4 <= i < 12:
                 leaf_stuffed(i - 4)
             if i == -1:
-                leaf_regroup(1)
                 leaf_quant()
             if live(i):
+                if i != last:
+                    pa_t[i] = pa_pool.tile([P, 4, R, P, 4], BF16, name="pa", align_bytes=64)
                 for r in range(R):
                     if i == last:
                         product_last(r)
                     else:
-                        product(i, r, path(i)[:, :, r])
+                        product(i, r, pa_t[i][:, :, r])
             if live(i + 1):
                 flip(i + 1, 0)
             if live(i + 2):
                 turn_rows(i + 2)
-            if live(i - 3):
+            if live(i - 3) and i - 3 < last - 1:
                 store(i - 3, 0)
             if live(i - 2) and i - 2 != last:
                 store(i - 2, 1)
-            if i == NBLK:
-                stage2_last(0)
+                if i - 2 == last - 1:
+                    store(i - 2, 0)
         stage2_last(1)

from contextlib import ExitStack

import concourse.mybir as mybir
from concourse.masks import make_identity

F32 = mybir.dt.float32
BF16 = mybir.dt.bfloat16
U32 = mybir.dt.uint32
I32 = mybir.dt.int32
U8 = mybir.dt.uint8
FP8X4 = mybir.dt.float8_e4m3fn_x4
ACT = mybir.ActivationFunctionType
ALU = mybir.AluOpType

P = 128
ROWS = 8192
FEAT = 512
DEPTH = 4
TREES = 64
LEAVES = 16
DOUT = 512
HALF = ROWS // 2
NB = 256
R = NB // P
CW = 2 * R * P
SW = CW // 4
RING = 5
NBLK = HALF // NB
PIN = True

FLOPS = 2 * ROWS * FEAT * DEPTH * TREES + 2 * ROWS * TREES * LEAVES * DOUT


def tile_neuralobliviousdecisiontree_t_kernel(tc, x, W, b, leaf_values, out):
    nc = tc.nc
    with ExitStack() as ctx:
        if PIN:
            ctx.enter_context(tc.manual_schedule())
        const = ctx.enter_context(tc.tile_pool(name="const", bufs=1))
        xr_pool = ctx.enter_context(tc.tile_pool(name="xr", bufs=4))
        pa_pool = ctx.enter_context(tc.tile_pool(name="pa", bufs=2))
        cx_pool = ctx.enter_context(tc.tile_pool(name="cx", bufs=2))
        q_pool = ctx.enter_context(tc.tile_pool(name="q", bufs=2))
        bb_pool = ctx.enter_context(tc.tile_pool(name="bb", bufs=2))
        o_pool = ctx.enter_context(tc.tile_pool(name="o", bufs=4))
        ps_x = ctx.enter_context(tc.psum_pool(name="psx", bufs=1))
        ps_z = ctx.enter_context(tc.psum_pool(name="psz", bufs=1))
        ps_a = ctx.enter_context(tc.psum_pool(name="psa", bufs=2))
        ps_o = ctx.enter_context(tc.psum_pool(name="pso", bufs=2))

        x_blk = x.rearrange("(h k p r) f -> k p h (r f)", h=2, k=NBLK, p=P, r=R)

        xr_t = {}
        pa_t = {}
        cx_t = {}
        z_t = {}
        pr_t = {}
        zt_t = {}
        qn_t = {}
        qk_t = {}
        bb_t = {}
        a2_t = {}
        o_t = {}

        def load_x(k):
            xr = xr_pool.tile([P, 2, R * FEAT], BF16, name="xr")
            xr_t[k] = xr
            if k > 0:
                nc.sync.dma_start(out=xr[:], in_=x_blk[k])

        def load_first(h):
            nc.sync.dma_start(out=xr_t[0][:, h], in_=x_blk[0][:, h])

        ident = const.tile([P, P], F32, name="ident")
        make_identity(nc, ident[:])

        wr = const.tile([P, DEPTH, 4, TREES], BF16, name="wr")
        bt = const.tile([P, P], BF16, name="bt")
        nc.gpsimd.memset(bt[:], 0.0)
        load_x(0)
        load_first(0)
        nc.sync.dma_start(
            out=wr[:].rearrange("q j (u e) t -> q (j u) (e t)", u=2, e=2),
            in_=W.rearrange("j (u q e) t -> q (j u) (e t)", u=2, q=P, e=2),
        )
        load_first(1)
        for n in range(2):
            nc.sync.dma_start(out=bt[0:DEPTH, n * TREES : (n + 1) * TREES], in_=b)
        nc.sync.dma_start(
            out=bt[DEPTH : DEPTH + 1, :], in_=b[2:4, :].rearrange("j t -> (j t)").unsqueeze(0)
        )
        lr = const.tile([P, LEAVES // 2, DOUT], BF16, name="lr")
        for u in range(2):
            nc.sync.dma_start(
                out=lr[u * TREES : (u + 1) * TREES],
                in_=leaf_values[:, u * 8 : (u + 1) * 8, :],
            )
        load_x(1)
        load_x(2)

        wg = const.tile([P, 2, 2, P, 4], BF16, name="wg", align_bytes=64)
        nc.gpsimd.memset(wg[:].rearrange("q v j m c -> q (v j m c)").bitcast(I32), 0)
        lc = const.tile([P, 2, DOUT], U32, name="lc", align_bytes=64)
        ls = const.tile([P, 2, DOUT], U8, name="ls", align_bytes=64)
        lz = const.tile([P, 2, 4, DOUT], U32, name="lz", align_bytes=64)
        lzs = const.tile([P, 2, 4, DOUT], U8, name="lzs", align_bytes=64)
        zero = const.tile([P, DOUT], U32, name="zero")
        nc.gpsimd.memset(zero[:].bitcast(I32), 0)
        nc.gpsimd.memset(ls[:].rearrange("p s d -> p (s d)").bitcast(I32), 0)
        pt_ring = []
        wt_ring = []
        for n in range(RING):
            pt = const.tile([P, 2 * CW + 2 * SW], U32, name=f"pt{n}", align_bytes=64)
            wt = const.tile([P, CW + SW], U32, name=f"wt{n}", align_bytes=64)
            nc.gpsimd.memset(pt[:, 2 * CW :].bitcast(I32), 0)
            pt_ring.append(pt)
            wt_ring.append(wt)

        ring = [const.tile([P, 4 * NB], F32, name=f"ring{n}", align_bytes=64) for n in range(3)]

        def grouped(k):
            return ring[k % 3][:].rearrange("q (h n u) -> q h n u", h=2, u=2)

        def rows_factor(k):
            return ring[(k + 1) % 3][:].rearrange("p (s c n) -> p s c n", s=2, c=2)

        wgn = const.tile([P, 2, TREES, 4], BF16, name="wgn", align_bytes=64)
        nc.vector.tensor_copy(out=wgn[:], in_=wr[:, 2:4].rearrange("q j c t -> q j t c"))
        for v in range(2):
            nc.vector.tensor_copy(
                out=wg[:, v, :, v * TREES : (v + 1) * TREES, :],
                in_=wr[:, 0:2].rearrange("q j c t -> q j t c"),
            )
        wcn = const.tile([P, 2 * TREES], U32, name="wcn", align_bytes=64)
        wsn = const.tile([P, 2 * TREES], U8, name="wsn", align_bytes=64)
        nc.vector.quantize_mx(
            out=wcn[:].bitcast(FP8X4),
            scales=wsn[:],
            in_=wgn[:].rearrange("q j t c -> q (j t c)"),
        )
        wc = const.tile([P, 4 * P], U32, name="wc", align_bytes=64)
        ws = const.tile([P, 4 * P], U8, name="ws", align_bytes=64)
        nc.vector.quantize_mx(
            out=wc[:].bitcast(FP8X4),
            scales=ws[:],
            in_=wg[:].rearrange("q v j m c -> q (v j m c)"),
        )

        bpos = const.tile([P, DEPTH + 1], F32, name="bpos")
        bneg = const.tile([P, DEPTH + 1], F32, name="bneg")

        def bias_columns():
            btf = const.tile([P, P], F32, name="btf")
            nc.vector.tensor_copy(out=btf[:], in_=bt[:])
            pb = ps_z.tile([P, P], F32, name="pb", tag="zt")
            nc.tensor.transpose(pb[:], btf[:], ident[:])
            nc.vector.tensor_copy(out=bpos[:], in_=pb[:, 0 : DEPTH + 1])
            nc.vector.tensor_scalar(
                out=bneg[:], in0=pb[:, 0 : DEPTH + 1], scalar1=-1.0, scalar2=None, op0=ALU.mult
            )

        lg = const.tile([P, 2, DOUT, 4], BF16, name="lg", align_bytes=64)

        def leaf_regroup(a):
            dst = lg[:, a].rearrange("p (c i) t -> p c t i", i=4)
            src = lr[:, 4 * a : 4 * a + 4, :].rearrange("p t (c i) -> p c t i", i=4)
            nc.vector.tensor_copy(out=dst, in_=src)

        def leaf_quant():
            nc.vector.quantize_mx(
                out=lc[:].rearrange("p a d -> p (a d)").bitcast(FP8X4),
                scales=ls[:].rearrange("p a d -> p (a d)"),
                in_=lg[:].rearrange("p a d i -> p (a d i)"),
            )

        last = NBLK - 1

        def transpose_x(k, h):
            xt = ps_x.tile([P, R, 2, P], F32, name="xt", tag="xt")
            xw = xr_t[k][:, h, :].bitcast(F32)
            for r in range(R):
                for u in range(2):
                    c0 = r * (FEAT // 2) + u * P
                    nc.tensor.transpose(xt[:, r, u, :], xw[:, c0 : c0 + P], ident[:])
            nc.scalar.copy(
                out=grouped(k)[:, h].rearrange("q (r p) u -> q r p u", r=R),
                in_=xt[:].rearrange("q r u p -> q r p u"),
            )

        def quant_x(k):
            cx = cx_pool.tile([P, 2, NB], U32, name="cx", align_bytes=64)
            sx = cx_pool.tile([P, 2, NB], U8, name="sx", align_bytes=64)
            nc.vector.quantize_mx(
                out=cx[:].rearrange("q h n -> q (h n)").bitcast(FP8X4),
                scales=sx[:].rearrange("q h n -> q (h n)"),
                in_=ring[k % 3][:].bitcast(BF16),
            )
            cx_t[k] = (cx, sx)

        def stage1_pe(k):
            cx, sx = cx_t[k]
            zr = ps_z.tile([P, 2 * NB], F32, name="zr", tag="zr")
            nc.tensor.matmul_mx(
                out=zr[:],
                lhsT=wcn[:].bitcast(FP8X4),
                lhsT_scale=wsn[:],
                rhs=cx[:].rearrange("q h n -> q (h n)").bitcast(FP8X4),
                rhs_scale=sx[:].rearrange("q h n -> q (h n)"),
                start=True,
                stop=True,
            )
            zk = ps_z.tile([P, 2, NB], F32, name="zk", tag="zk")
            for jj in range(2):
                for v in range(2):
                    w0 = (v * 2 + jj) * P
                    nc.tensor.matmul_mx(
                        out=zk[:, jj, :],
                        lhsT=wc[:, w0 : w0 + P].bitcast(FP8X4),
                        lhsT_scale=ws[:, w0 : w0 + P],
                        rhs=cx[:, v, :].bitcast(FP8X4),
                        rhs_scale=sx[:, v, :],
                        start=(v == 0),
                        stop=(v == 1),
                    )
            z_t[k] = (zr, zk)

        def sigmoid_rows(k):
            pr = q_pool.tile([P, 2 * NB], F32, name="pr")
            nc.scalar.activation(
                out=pr[:], in_=z_t[k][0][:], func=ACT.Sigmoid,
                bias=bpos[:, DEPTH : DEPTH + 1], scale=1.0,
            )
            pr_t[k] = pr

        def turn_rows(k):
            zt = ps_z.tile([P, 2 * R, 2, TREES], F32, name="zt", tag="zt")
            for r in range(R):
                for h in range(2):
                    c0 = h * NB + r * P
                    nc.tensor.transpose(
                        zt[:, 2 * r + h].rearrange("p j t -> p (j t)"),
                        pr_t[k][:, c0 : c0 + P],
                        ident[:],
                    )
            zt_t[k] = zt

        def rows_out(k):
            zt = zt_t[k][:].rearrange("p g j t -> p j g t")
            qn = q_pool.tile([P, 2, 2, 2 * R, TREES], F32, name="qn")
            nc.scalar.activation(out=qn[:, 0], in_=zt, func=ACT.Copy)
            nc.scalar.activation(out=qn[:, 1], in_=zt, func=ACT.Copy, scale=-1.0, bias=1.0)
            qn_t[k] = qn

        def sigmoid_cols(k):
            zk = z_t[k][1]
            qk = q_pool.tile([P, 2, 2, NB], F32, name="qk")
            for j in range(2):
                nc.scalar.activation(
                    out=qk[:, j, 0, :], in_=zk[:, j, :], func=ACT.Sigmoid,
                    bias=bpos[:, j : j + 1], scale=1.0,
                )
                nc.scalar.activation(
                    out=qk[:, j, 1, :], in_=zk[:, j, :], func=ACT.Sigmoid,
                    bias=bneg[:, j : j + 1], scale=-1.0,
                )
            qk_t[k] = qk

        def factors(k):
            eng = nc.vector if k == 0 else nc.gpsimd
            qn = qn_t[k][:].rearrange("p s j g t -> p s j (g t)")
            eng.tensor_tensor(
                out=rows_factor(k),
                in0=qn[:, :, 0].unsqueeze(2).to_broadcast([P, 2, 2, NB]),
                in1=qn[:, :, 1].unsqueeze(1).to_broadcast([P, 2, 2, NB]),
                op=ALU.mult,
            )
            bb = bb_pool.tile([P, 2, 2, NB], F32, name="bb")
            qk = qk_t[k]
            eng.tensor_tensor(
                out=bb[:],
                in0=qk[:, 0].unsqueeze(2).to_broadcast([P, 2, 2, NB]),
                in1=qk[:, 1].unsqueeze(1).to_broadcast([P, 2, 2, NB]),
                op=ALU.mult,
            )
            bb_t[k] = bb

        def flip(k, r):
            a2 = ps_a.tile([P, P, 4], F32, name="a2")
            for a in range(4):
                nc.tensor.transpose(
                    a2[:, :, a],
                    rows_factor(k)[:, a // 2, a % 2, r * P : (r + 1) * P],
                    ident[:],
                )
            a2_t[(k, r)] = a2

        def product(k, r, dst, groups=slice(0, 4)):
            shape = [P, groups.stop - groups.start, P, 4]
            nc.vector.tensor_tensor(
                out=dst,
                in0=a2_t[(k, r)][:].unsqueeze(1).to_broadcast(shape),
                in1=bb_t[k][:].rearrange("p s c n -> p (s c) n")[:, groups, r * P : (r + 1) * P]
                .unsqueeze(3).to_broadcast(shape),
                op=ALU.mult,
            )

        def quant_path(k):
            pt = pt_ring[k % RING]
            nc.vector.quantize_mx(
                out=pt[:, 0 : 2 * CW].bitcast(FP8X4),
                scales=pt[:, 2 * CW :].bitcast(U8),
                in_=pa_t[k][:].rearrange("p a r n i -> p (a r n i)"),
            )

        lo = slice(0, TREES)
        hi = slice(TREES, 2 * TREES)
        first = (slice(0, CW), slice(2 * CW, 2 * CW + SW))
        second = (slice(CW, 2 * CW), slice(2 * CW + SW, 2 * CW + 2 * SW))
        packed = (slice(0, CW), slice(CW, CW + SW))

        def gather(k):
            pt = pt_ring[k % RING][:].bitcast(I32)
            wt = wt_ring[k % RING][:].bitcast(I32)
            for n in range(2):
                nc.sync.dma_start(out=wt[lo, packed[n]], in_=pt[hi, first[n]])
                nc.sync.dma_start(out=wt[hi, packed[n]], in_=pt[hi, second[n]])

        own_t = {}

        def gather_rest(k):
            pt = pt_ring[k % RING][:].bitcast(I32)
            if k < last - 1:
                for n in range(2):
                    nc.sync.dma_start(out=pt[hi, first[n]], in_=pt[lo, second[n]])
                return
            own_t[k] = wt_ring[(k + 1) % RING]
            at = own_t[k][:].bitcast(I32)
            for n in range(2):
                nc.sync.dma_start(out=at[lo, packed[n]], in_=pt[lo, first[n]])
                nc.sync.dma_start(out=at[hi, packed[n]], in_=pt[lo, second[n]])

        def stage2(k, h):
            if h == 1 or k in own_t:
                src = wt_ring[k % RING] if h == 1 else own_t[k]
                scales = src[:, packed[1]].bitcast(U8)
            else:
                src = pt_ring[k % RING]
                scales = src[:, first[1]].bitcast(U8)
            o = o_pool.tile([P, R, DOUT], F32, name="o")
            for r in range(R):
                acc = ps_o.tile([P, DOUT], F32, name="acc")
                for s in range(2):
                    c0 = (s * R + r) * P
                    nc.tensor.matmul_mx(
                        out=acc[:],
                        lhsT=src[:, c0 : c0 + P].bitcast(FP8X4),
                        lhsT_scale=scales[:, c0 : c0 + P],
                        rhs=lc[:, s, :].bitcast(FP8X4),
                        rhs_scale=ls[:, s, :],
                        start=(s == 0),
                        stop=(s == 1),
                    )
                if k == last - 1 and h == 0:
                    nc.vector.tensor_scalar(
                        out=o[:, r, :], in0=acc[:], scalar1=1.0 / TREES, scalar2=None, op0=ALU.mult
                    )
                else:
                    nc.scalar.activation(
                        out=o[:, r, :], in_=acc[:], func=ACT.Copy, scale=1.0 / TREES
                    )
            o_t[(k, h)] = o

        def store(k, h):
            row0 = h * HALF + k * NB
            nc.sync.dma_start(
                out=out[row0 : row0 + NB, :].rearrange("(p r) d -> p r d", r=R),
                in_=o_t[(k, h)][:],
            )

        def leaf_stuffed(step):
            h, n = divmod(step, 4)
            halves = (slice(0, TREES), slice(TREES, 2 * TREES))
            this, other = halves[h], halves[1 - h]
            scales = lzs[:].rearrange("p h a d -> p h (a d)").bitcast(I32)
            one = ls[:].rearrange("p s d -> p (s d)").bitcast(I32)
            if n < 2:
                src = zero[other, :].bitcast(I32).unsqueeze(1).to_broadcast([TREES, 2, DOUT])
                nc.sync.dma_start(out=lz[other, h, 2 * n : 2 * n + 2, :].bitcast(I32), in_=src)
                if n == 0:
                    nc.sync.dma_start(out=scales[other, h], in_=zero[other, :].bitcast(I32))
            else:
                u = n - 2
                nc.sync.dma_start(
                    out=lz[this, h, 2 * u : 2 * u + 2, :].bitcast(I32),
                    in_=lc[halves[u], :, :].bitcast(I32),
                )
                nc.sync.dma_start(
                    out=scales[this, h, u * (DOUT // 2) : (u + 1) * (DOUT // 2)],
                    in_=one[halves[u], :],
                )

        pl_t = {}

        def product_last(r):
            pl = const.tile([P, 4, P, 4], BF16, name=f"pl{r}", align_bytes=64)
            ql = const.tile([P, 4, P], U32, name=f"ql{r}", align_bytes=64)
            sl = const.tile([P, 4, P], U8, name=f"sl{r}", align_bytes=64)
            pl_t[r] = (ql, sl)
            parts = [slice(0, 4)] if r == 0 else [slice(0, 2), slice(2, 4)]
            for part in parts:
                product(last, r, pl[:, part], part)
            for part in parts:
                nc.vector.quantize_mx(
                    out=ql[:, part].rearrange("p a n -> p (a n)").bitcast(FP8X4),
                    scales=sl[:, part].rearrange("p a n -> p (a n)"),
                    in_=pl[:, part].rearrange("p a n i -> p (a n i)"),
                )

        def stage2_last(r):
            ql, sl = pl_t[r]
            accs = []
            for h in range(2):
                tag = (("zr", "zk"), ("zt", "xt"))[r][h]
                bank = ps_x if tag == "xt" else ps_z
                accs.append(bank.tile([P, DOUT], F32, name="acc_last", tag=tag))
            for part in ([range(0, 4)] if r == 0 else [range(0, 2), range(2, 4)]):
                for h in range(2):
                    for a in part:
                        nc.tensor.matmul_mx(
                            out=accs[h][:],
                            lhsT=ql[:, a, :].bitcast(FP8X4),
                            lhsT_scale=sl[:, a, :],
                            rhs=lz[:, h, a, :].bitcast(FP8X4),
                            rhs_scale=lzs[:, h, a, :],
                            start=(a == 0),
                            stop=(a == 3),
                        )
            for h in range(2):
                acc = accs[h]
                ol = o_pool.tile([P, DOUT], F32, name="ol")
                if h == 1:
                    nc.vector.tensor_scalar(
                        out=ol[:], in0=acc[:], scalar1=1.0 / TREES, scalar2=None, op0=ALU.mult
                    )
                else:
                    nc.scalar.activation(out=ol[:], in_=acc[:], func=ACT.Copy, scale=1.0 / TREES)
                row0 = h * HALF + last * NB
                nc.sync.dma_start(
                    out=out[row0 : row0 + NB, :].rearrange("(p r) d -> p r d", r=R)[:, r],
                    in_=ol[:],
                )

        def live(k):
            return 0 <= k < NBLK

        for i in range(-3, NBLK + 1):
            if 3 <= i + 6 < NBLK:
                load_x(i + 6)
            if live(i - 2) and i - 2 < last - 1:
                gather_rest(i - 2)
            if live(i + 1):
                rows_out(i + 1)
            if live(i):
                flip(i, 1)
            if live(i + 3):
                transpose_x(i + 3, 0)
            if i == -3:
                bias_columns()
            if live(i + 2):
                quant_x(i + 2)
                stage1_pe(i + 2)
                sigmoid_rows(i + 2)
            if live(i - 3) and i - 3 < last - 1:
                stage2(i - 3, 0)
            if live(i + 2):
                sigmoid_cols(i + 2)
            if live(i + 3):
                transpose_x(i + 3, 1)
            if i == NBLK:
                stage2_last(0)
            if live(i - 2) and i - 2 != last:
                stage2(i - 2, 1)
                if i - 2 == last - 1:
                    stage2(i - 2, 0)
            if i == -2:
                leaf_regroup(0)
                leaf_regroup(1)
            if live(i - 1) and i - 1 != last:
                quant_path(i - 1)
                gather(i - 1)
                if i - 1 == last - 1:
                    gather_rest(i - 1)
            if live(i + 1):
                factors(i + 1)
            if 4 <= i < 12:
                leaf_stuffed(i - 4)
            if i == -1:
                leaf_quant()
            if live(i):
                if i != last:
                    pa_t[i] = pa_pool.tile([P, 4, R, P, 4], BF16, name="pa", align_bytes=64)
                for r in range(R):
                    if i == last:
                        product_last(r)
                    else:
                        product(i, r, pa_t[i][:, :, r])
            if live(i + 1):
                flip(i + 1, 0)
            if live(i + 2):
                turn_rows(i + 2)
            if live(i - 3) and i - 3 < last - 1:
                store(i - 3, 0)
            if live(i - 2) and i - 2 != last:
                store(i - 2, 1)
                if i - 2 == last - 1:
                    store(i - 2, 0)
        stage2_last(1)
